import numpy as np
import ml_dtypes


def mxq(x, axis, fmt="e4m3"):
    dtype, down = {"e4m3": (ml_dtypes.float8_e4m3fn, 7), "e5m2": (ml_dtypes.float8_e5m2, 14)}[fmt]
    v = np.moveaxis(np.asarray(x, np.float32).astype(ml_dtypes.bfloat16).astype(np.float64), axis, -1)
    blocks = v.reshape(v.shape[:-1] + (-1, 32))
    amax = np.abs(blocks).max(-1, keepdims=True)
    byte = np.maximum(np.where(amax > 0, np.frexp(amax)[1] - 1 + 127, 0) - down, 1)
    scale = np.exp2(byte - 127.0)
    codes = (blocks / scale).astype(np.float32).astype(dtype).astype(np.float64)
    return np.moveaxis((codes * scale).reshape(v.shape), -1, axis)


WIDE = False


def mx_kscale(k):
    if not WIDE:
        return np.ones(k)
    levels = np.array([10, -10, 5, -5, 0])
    a = np.random.permutation(np.resize(levels, k // 512 * 4)).reshape(k // 512, 4)
    idx = np.arange(k)
    return np.exp2(a[idx // 512, idx % 128 // 32])


BF16 = ml_dtypes.bfloat16


def bf(x):
    return np.asarray(x, np.float32).astype(BF16)


def f64(x):
    return np.asarray(x).astype(np.float64)


B, D_IN, D_OUT = 1024, 1024, 1024


def sigmoid(v):
    return 1.0 / (1.0 + np.exp(-v))


def setup_inputs():
    s, t = mx_kscale(D_IN), mx_kscale(D_OUT)

    def wx():
        return bf(np.random.standard_normal((D_IN, D_OUT)) / np.sqrt(D_IN) / s[:, None])

    def wh():
        return bf(np.random.standard_normal((D_OUT, D_OUT)) / np.sqrt(D_OUT) / t[:, None])

    return {"x": bf(np.random.standard_normal((B, D_IN)) * s),
            "hist": bf(np.random.standard_normal((B, D_OUT)) * t),
            "Wix": wx(), "Wih": wh(), "b_i": bf(np.random.standard_normal(D_OUT) * 0.3),
            "Wcx": wx(), "Wch": wh(), "b_c": bf(np.random.standard_normal(D_OUT) * 0.3)}


def reference(x, hist, Wix, Wih, b_i, Wcx, Wch, b_c):
    xq = mxq(f64(x), 1, "e4m3")
    hq = mxq(f64(hist), 1, "e4m3")
    i = sigmoid((xq @ mxq(f64(Wix), 0, "e4m3")) + (hq @ mxq(f64(Wih), 0, "e4m3")) + f64(b_i))
    g = np.tanh((xq @ mxq(f64(Wcx), 0, "e4m3")) + (hq @ mxq(f64(Wch), 0, "e4m3")) + f64(b_c))
    return i * g

@@ -1,0 +1,258 @@
+from contextlib import ExitStack
+
+import concourse.bass as bass
+import concourse.mybir as mybir
+import concourse.tile as tile
+from concourse.masks import make_identity
+
+F32 = mybir.dt.float32
+BF16 = mybir.dt.bfloat16
+U32 = mybir.dt.uint32
+U8 = mybir.dt.uint8
+I32 = mybir.dt.int32
+FP8X4 = mybir.dt.float8_e4m3fn_x4
+ACT = mybir.ActivationFunctionType
+ALU = mybir.AluOpType
+
+P = 128
+FLOPS = 2 * 1024 * 2048 * 2048
+
+FORM = {(0, 0): "B", (0, 1): "B", (1, 0): "B", (1, 1): "A"}
+S_REGROUP = ((1, 1), (2, 1), (3, 1), (4, 1), (5, 1))
+V_XCOPY = (2, 5, 8, 11, 14)
+PIN = False
+
+
+def tile_lstmmirrored_pa_kernel(tc, x, hist, Wix, Wih, b_i, Wcx, Wch, b_c, out):
+    nc = tc.nc
+    with ExitStack() as ctx:
+        if PIN:
+            ctx.enter_context(tc.manual_schedule())
+        const = ctx.enter_context(tc.tile_pool(name="const", bufs=1))
+        keep = ctx.enter_context(tc.tile_pool(name="keep", bufs=1))
+        raw = ctx.enter_context(tc.tile_pool(name="raw", bufs=8))
+        grp = ctx.enter_context(tc.tile_pool(name="grp", bufs=5))
+        spool = ctx.enter_context(tc.tile_pool(name="spool", bufs=12))
+        gpool = ctx.enter_context(tc.tile_pool(name="gpool", bufs=3))
+        upool = ctx.enter_context(tc.tile_pool(name="upool", bufs=3))
+        stpool = ctx.enter_context(tc.tile_pool(name="stpool", bufs=2))
+        psum = ctx.enter_context(tc.psum_pool(name="psum", bufs=8))
+
+        xv = x.rearrange("(p t) k -> p (t k)", t=8)
+        hv = hist.rearrange("(p t) k -> p (t k)", t=8)
+        ov = out.rearrange("(p t) n -> p t n", t=8)
+        mats = ((Wix, Wih), (Wcx, Wch))
+        hcs = [(nh, gate, part) for nh in range(2) for gate in range(2) for part in range(2)]
+
+        warm = const.tile([P, 1], F32, name="warm")
+        nc.vector.memset(warm[:], 0.0)
+        nc.scalar.activation(out=warm[:], in_=warm[:], func=ACT.Sigmoid)
+        ident = const.tile([P, P], F32, name="ident")
+        make_identity(nc, ident[:])
+        brow = const.tile([P, P], BF16, name="brow")
+        nc.vector.memset(brow[:], 0.0)
+        nc.scalar.dma_start(out=brow[0:8, :], in_=b_i.rearrange("(j n) -> j n", n=P))
+        nc.scalar.dma_start(out=brow[8:16, :], in_=b_c.rearrange("(j n) -> j n", n=P))
+        zrow = const.tile([P, 2048], BF16, name="zrow")
+        nc.vector.memset(zrow[:].bitcast(I32), 0)
+        nc.scalar.dma_start(out=zrow[0:1, 0:1024], in_=b_i.rearrange("(o n) -> o n", o=1))
+        nc.scalar.dma_start(out=zrow[0:1, 1024:2048], in_=b_c.rearrange("(o n) -> o n", o=1))
+        ones = const.tile([P, P], BF16, name="ones")
+        nc.vector.memset(ones[:], 1.0)
+
+        xq = keep.tile([P, 4 * 1024], U32, name="xq", align_bytes=64)
+        xs = keep.tile([P, 4 * 1024], U8, name="xs", align_bytes=64)
+        wq = keep.tile([P, 8 * 1024], U32, name="wq", align_bytes=64)
+        ws = keep.tile([P, 8 * 1024], U8, name="ws", align_bytes=64)
+
+        xraw = []
+        for si, v in enumerate((xv, hv)):
+            for hh in range(2):
+                r = raw.tile([P, 4096], BF16, name="xr%d%d" % (si, hh), tag="raw")
+                for a in range(2):
+                    lo = (hh * 4 + a * 2) * 1024
+                    nc.sync.dma_start(out=r[:, a * 2048:(a + 1) * 2048], in_=v[:, lo:lo + 2048])
+                xraw.append(r)
+
+        wraw = {}
+
+        def load_w(k):
+            nh, gate, part = hcs[k]
+            wv = mats[gate][part][:, nh * 512:(nh + 1) * 512].rearrange("(a q e) c -> q a e c", a=4, e=2)
+            r = raw.tile([P, 4096], BF16, name="wr%d" % k, tag="raw")
+            rv = r[:].rearrange("q (a e c) -> q a e c", a=4, e=2)
+            if k == 0:
+                for a in range(4):
+                    nc.sync.dma_start(out=rv[:, a, :, :], in_=wv[:, a, :, :])
+            else:
+                for e in range(2):
+                    nc.sync.dma_start(out=rv[:, :, e, :], in_=wv[:, :, e, :])
+            wraw[k] = r
+
+        for k in range(4):
+            load_w(k)
+
+        gx = {}
+
+        def x_block(si, tp):
+            rf = xraw[si * 2 + tp // 2][:].bitcast(F32)
+            h = tp // 2
+            for g in range(2):
+                bk = psum.tile([P, 512], F32, name="bkx", tag="bank")
+                for u in range(2):
+                    for t2 in range(2):
+                        w0 = ((tp % 2) * 2 + t2) * 512 + (2 * g + u) * P
+                        o0 = (u * 2 + t2) * P
+                        nc.tensor.transpose(bk[:, o0:o0 + P], rf[:, w0:w0 + P], ident[:])
+                c = 2 * si + g
+                if tp % 2 == 0:
+                    gx[(c, h)] = grp.tile([P, 2048], BF16, name="gx%d%d" % (c, h), tag="grp", align_bytes=64)
+                dst = gx[(c, h)][:].bitcast(F32).rearrange("q (c u) -> q c u", u=2)
+                dst = dst[:, (tp % 2) * 256:(tp % 2) * 256 + 256, :]
+                srcv = bk[:].rearrange("q (u c) -> q c u", u=2)
+                if (si * 8 + tp * 2 + g) in V_XCOPY:
+                    nc.vector.tensor_copy(out=dst, in_=srcv)
+                else:
+                    nc.scalar.copy(out=dst, in_=srcv)
+            if tp % 2 == 1:
+                for g in range(2):
+                    c = 2 * si + g
+                    lo = c * 1024 + h * 512
+                    nc.vector.quantize_mx(
+                        out=xq[:, lo:lo + 512].bitcast(FP8X4),
+                        scales=xs[:, lo:lo + 512],
+                        in_=gx[(c, h)][:],
+                    )
+
+        for tp in range(4):
+            x_block(0, tp)
+
+        browf = const.tile([P, P], F32, name="browf")
+        nc.vector.tensor_copy(out=browf[:], in_=brow[:])
+        bkb = psum.tile([P, 512], F32, name="bkb", tag="bank")
+        nc.tensor.transpose(bkb[:, 0:P], browf[:], ident[:])
+        bT = const.tile([P, 16], F32, name="bT")
+        nc.vector.tensor_copy(out=bT[:], in_=bkb[:, 0:16])
+        bb = const.tile([P, 2048], F32, name="bb")
+        for gate in range(2):
+            for nh in range(2):
+                if "A" in (FORM[(nh, 0)], FORM[(nh, 1)]):
+                    lo = gate * 1024 + nh * 512
+                    bko = psum.tile([P, 512], F32, name="bko", tag="bank")
+                    nc.tensor.matmul(bko[:], lhsT=ones[:], rhs=zrow[:, lo:lo + 512], start=True, stop=True)
+                    nc.vector.tensor_copy(out=bb[:, lo:lo + 512], in_=bko[:])
+
+        for tp in range(4):
+            x_block(1, tp)
+
+        for k in range(4, 8):
+            load_w(k)
+
+        def prep_w(k):
+            nh, gate, part = hcs[k]
+            for g in range(2):
+                gw = grp.tile([P, 2048], BF16, name="gw%d%d" % (k, g), tag="grp", align_bytes=64)
+                dst = gw[:].rearrange("q (c i t) -> q c t i", i=4, t=4)
+                srcv = wraw[k][:, g * 2048:(g + 1) * 2048].rearrange("q (t c i) -> q c t i", t=4, i=4)
+                if (k, g) in S_REGROUP:
+                    nc.scalar.copy(out=dst, in_=srcv)
+                else:
+                    nc.vector.tensor_copy(out=dst, in_=srcv)
+                lo = (gate * 4 + part * 2 + g) * 1024 + nh * 512
+                nc.vector.quantize_mx(
+                    out=wq[:, lo:lo + 512].bitcast(FP8X4),
+                    scales=ws[:, lo:lo + 512],
+                    in_=gw[:],
+                )
+
+        banks = {}
+        s_t = {}
+        st = {}
+
+        def mx(nh, gate, h, i, c):
+            wl = (gate * 4 + c) * 1024 + nh * 512
+            if FORM[(nh, h)] == "B":
+                a, b = wl + i * P, c * 1024 + h * 512
+                l_c, l_s, r_c, r_s = wq, ws, xq, xs
+            else:
+                a, b = c * 1024 + (h * 4 + i) * P, wl
+                l_c, l_s, r_c, r_s = xq, xs, wq, ws
+            nc.tensor.matmul_mx(
+                out=banks[(h, i)][:],
+                lhsT=l_c[:, a:a + P].bitcast(FP8X4),
+                lhsT_scale=l_s[:, a:a + P],
+                rhs=r_c[:, b:b + 512].bitcast(FP8X4),
+                rhs_scale=r_s[:, b:b + 512],
+                start=(c == 0),
+                stop=(c == 3),
+            )
+
+        def store(nh, h, a):
+            nc.sync.dma_start(
+                out=ov[:, h * 4 + 2 * a:h * 4 + 2 * a + 2, nh * 512:(nh + 1) * 512],
+                in_=st[h][:, 2 * a:2 * a + 2, :],
+            )
+
+        def close(nh, gate, h, i):
+            bank = banks[(h, i)]
+            func = ACT.Sigmoid if gate == 0 else ACT.Tanh
+            if gate == 0:
+                s_t[(h, i)] = spool.tile([P, 512], F32, name="s", tag="s")
+                dst = s_t[(h, i)]
+            else:
+                dst = gpool.tile([P, 512], F32, name="gt", tag="gt")
+            if FORM[(nh, h)] == "B":
+                col = gate * 8 + nh * 4 + i
+                nc.scalar.activation(out=dst[:], in_=bank[:], func=func, bias=bT[:, col:col + 1])
+            else:
+                lo = gate * 1024 + nh * 512
+                u = upool.tile([P, 512], F32, name="u", tag="u")
+                nc.vector.tensor_tensor(out=u[:], in0=bank[:], in1=bb[:, lo:lo + 512], op=ALU.add)
+                nc.scalar.activation(out=dst[:], in_=u[:], func=func)
+            if gate == 1:
+                s = s_t[(h, i)]
+                if FORM[(nh, h)] == "B":
+                    nc.vector.tensor_tensor(out=s[:], in0=s[:], in1=dst[:], op=ALU.mult)
+                else:
+                    nc.vector.tensor_tensor(out=st[h][:, i, :], in0=s[:], in1=dst[:], op=ALU.mult)
+                    if i % 2 == 1:
+                        store(nh, h, i // 2)
+
+        def turn_back(nh, h):
+            for tl in range(4):
+                bt = psum.tile([P, 512], F32, name="bt", tag="bank")
+                for i in range(4):
+                    nc.tensor.transpose(bt[:, i * P:(i + 1) * P], s_t[(h, i)][:, tl * P:(tl + 1) * P], ident[:])
+                if tl % 2 == 0:
+                    nc.scalar.copy(out=st[h][:, tl, :], in_=bt[:])
+                else:
+                    nc.vector.tensor_copy(out=st[h][:, tl, :], in_=bt[:])
+                    store(nh, h, tl // 2)
+
+        groups = [(h, i) for h in range(2) for i in range(4)]
+        prep_w(0)
+        prep_w(1)
+        for k in range(8):
+            nh, gate, part = hcs[k]
+            if k + 2 < 8:
+                prep_w(k + 2)
+            if part == 0:
+                for h, i in groups:
+                    banks[(h, i)] = psum.tile([P, 512], F32, name="acc", tag="bank")
+            if gate == 1 and part == 1:
+                for h in range(2):
+                    st[h] = stpool.tile([P, 4, 512], F32, name="st", tag="st")
+            if k == 0:
+                for c in range(2):
+                    for h, i in groups:
+                        mx(nh, gate, h, i, c)
+            else:
+                for h, i in groups:
+                    for c in (2 * part, 2 * part + 1):
+                        mx(nh, gate, h, i, c)
+                    if part == 1:
+                        close(nh, gate, h, i)
+            if gate == 1 and part == 1:
+                for h in range(2):
+                    if FORM[(nh, h)] == "B":
+                        turn_back(nh, h)

@@ -17,10 +17,17 @@ ALU = mybir.AluOpType
 P = 128
 FLOPS = 2 * 1024 * 2048 * 2048
 
-FORM = {(0, 0): "B", (0, 1): "B", (1, 0): "B", (1, 1): "A"}
-S_REGROUP = ((1, 1), (2, 1), (3, 1), (4, 1), (5, 1))
-V_XCOPY = (2, 5, 8, 11, 14)
-PIN = False
+FORM = {(0, 0): "B", (0, 1): "B", (1, 0): "A", (1, 1): "A"}
+S_REGROUP = ((1, 0), (1, 1), (3, 0), (4, 0), (5, 0), (6, 0))
+V_XCOPY = (1, 3, 5, 7)
+SPLIT = ((0, 0), (0, 1))
+G_PROD = ()
+PREP_AT = {2: 0, 3: 8, 4: 16, 5: 24, 6: 34, 7: 38}
+LAG1 = 1
+LAG2 = 2
+TLAG = 2
+T_ON_V = (1, 3)
+PIN = True
 
 
 def tile_lstmmirrored_pa_kernel(tc, x, hist, Wix, Wih, b_i, Wcx, Wch, b_c, out):
@@ -31,7 +38,7 @@ def tile_lstmmirrored_pa_kernel(tc, x, hist, Wix, Wih, b_i, Wcx, Wch, b_c, out):
         const = ctx.enter_context(tc.tile_pool(name="const", bufs=1))
         keep = ctx.enter_context(tc.tile_pool(name="keep", bufs=1))
         raw = ctx.enter_context(tc.tile_pool(name="raw", bufs=8))
-        grp = ctx.enter_context(tc.tile_pool(name="grp", bufs=5))
+        grp = ctx.enter_context(tc.tile_pool(name="grp", bufs=8))
         spool = ctx.enter_context(tc.tile_pool(name="spool", bufs=12))
         gpool = ctx.enter_context(tc.tile_pool(name="gpool", bufs=3))
         upool = ctx.enter_context(tc.tile_pool(name="upool", bufs=3))
@@ -49,10 +56,6 @@ def tile_lstmmirrored_pa_kernel(tc, x, hist, Wix, Wih, b_i, Wcx, Wch, b_c, out):
         nc.scalar.activation(out=warm[:], in_=warm[:], func=ACT.Sigmoid)
         ident = const.tile([P, P], F32, name="ident")
         make_identity(nc, ident[:])
-        brow = const.tile([P, P], BF16, name="brow")
-        nc.vector.memset(brow[:], 0.0)
-        nc.scalar.dma_start(out=brow[0:8, :], in_=b_i.rearrange("(j n) -> j n", n=P))
-        nc.scalar.dma_start(out=brow[8:16, :], in_=b_c.rearrange("(j n) -> j n", n=P))
         zrow = const.tile([P, 2048], BF16, name="zrow")
         nc.vector.memset(zrow[:].bitcast(I32), 0)
         nc.scalar.dma_start(out=zrow[0:1, 0:1024], in_=b_i.rearrange("(o n) -> o n", o=1))
@@ -81,7 +84,7 @@ def tile_lstmmirrored_pa_kernel(tc, x, hist, Wix, Wih, b_i, Wcx, Wch, b_c, out):
             wv = mats[gate][part][:, nh * 512:(nh + 1) * 512].rearrange("(a q e) c -> q a e c", a=4, e=2)
             r = raw.tile([P, 4096], BF16, name="wr%d" % k, tag="raw")
             rv = r[:].rearrange("q (a e c) -> q a e c", a=4, e=2)
-            if k == 0:
+            if k < 2:
                 for a in range(4):
                     nc.sync.dma_start(out=rv[:, a, :, :], in_=wv[:, a, :, :])
             else:
@@ -114,56 +117,76 @@ def tile_lstmmirrored_pa_kernel(tc, x, hist, Wix, Wih, b_i, Wcx, Wch, b_c, out):
                     nc.vector.tensor_copy(out=dst, in_=srcv)
                 else:
                     nc.scalar.copy(out=dst, in_=srcv)
-            if tp % 2 == 1:
-                for g in range(2):
-                    c = 2 * si + g
-                    lo = c * 1024 + h * 512
-                    nc.vector.quantize_mx(
-                        out=xq[:, lo:lo + 512].bitcast(FP8X4),
-                        scales=xs[:, lo:lo + 512],
-                        in_=gx[(c, h)][:],
-                    )
 
-        for tp in range(4):
-            x_block(0, tp)
+        def x_quant(si, h):
+            for g in range(2):
+                c = 2 * si + g
+                lo = c * 1024 + h * 512
+                nc.vector.quantize_mx(
+                    out=xq[:, lo:lo + 512].bitcast(FP8X4),
+                    scales=xs[:, lo:lo + 512],
+                    in_=gx[(c, h)][:],
+                )
 
-        browf = const.tile([P, P], F32, name="browf")
-        nc.vector.tensor_copy(out=browf[:], in_=brow[:])
-        bkb = psum.tile([P, 512], F32, name="bkb", tag="bank")
-        nc.tensor.transpose(bkb[:, 0:P], browf[:], ident[:])
+        def bias_prep():
+            bkb = psum.tile([P, 512], F32, name="bkb", tag="bank")
+            for col in range(16):
+                nc.tensor.matmul(bkb[:, col * 32:(col + 1) * 32], lhsT=zrow[:, col * P:(col + 1) * P], rhs=ones[:, 0:32],
+                                 start=True, stop=True)
+            nc.scalar.copy(out=bT[:], in_=bkb[:].rearrange("p (c r) -> p c r", r=32)[:, :, 0])
+            for gate in range(2):
+                for nh in range(2):
+                    if "A" in (FORM[(nh, 0)], FORM[(nh, 1)]):
+                        lo = gate * 1024 + nh * 512
+                        bko = psum.tile([P, 512], F32, name="bko", tag="bank")
+                        nc.tensor.matmul(bko[:], lhsT=ones[:], rhs=zrow[:, lo:lo + 512], start=True, stop=True)
+                        nc.scalar.copy(out=bb[:, lo:lo + 512], in_=bko[:])
+
         bT = const.tile([P, 16], F32, name="bT")
-        nc.vector.tensor_copy(out=bT[:], in_=bkb[:, 0:16])
         bb = const.tile([P, 2048], F32, name="bb")
-        for gate in range(2):
-            for nh in range(2):
-                if "A" in (FORM[(nh, 0)], FORM[(nh, 1)]):
-                    lo = gate * 1024 + nh * 512
-                    bko = psum.tile([P, 512], F32, name="bko", tag="bank")
-                    nc.tensor.matmul(bko[:], lhsT=ones[:], rhs=zrow[:, lo:lo + 512], start=True, stop=True)
-                    nc.vector.tensor_copy(out=bb[:, lo:lo + 512], in_=bko[:])
 
-        for tp in range(4):
-            x_block(1, tp)
+        for si in range(2):
+            for tp in range(4):
+                x_block(si, tp)
+                if (si, tp) in ((0, 2), (1, 0), (1, 2)):
+                    x_quant((si * 4 + tp - 2) // 4, ((si * 4 + tp - 2) % 4) // 2)
 
+        bias_prep()
         for k in range(4, 8):
             load_w(k)
 
         def prep_w(k):
             nh, gate, part = hcs[k]
-            for g in range(2):
-                gw = grp.tile([P, 2048], BF16, name="gw%d%d" % (k, g), tag="grp", align_bytes=64)
-                dst = gw[:].rearrange("q (c i t) -> q c t i", i=4, t=4)
+            gw = {}
+
+            def regroup(g):
+                gw[g] = grp.tile([P, 2048], BF16, name="gw%d%d" % (k, g), tag="grp", align_bytes=64)
+                dst = gw[g][:].rearrange("q (c i t) -> q c t i", i=4, t=4)
                 srcv = wraw[k][:, g * 2048:(g + 1) * 2048].rearrange("q (t c i) -> q c t i", t=4, i=4)
                 if (k, g) in S_REGROUP:
                     nc.scalar.copy(out=dst, in_=srcv)
                 else:
                     nc.vector.tensor_copy(out=dst, in_=srcv)
+
+            def quant(g):
                 lo = (gate * 4 + part * 2 + g) * 1024 + nh * 512
                 nc.vector.quantize_mx(
                     out=wq[:, lo:lo + 512].bitcast(FP8X4),
                     scales=ws[:, lo:lo + 512],
-                    in_=gw[:],
+                    in_=gw[g][:],
                 )
+
+            if k == 0:
+                regroup(0)
+                quant(0)
+                regroup(1)
+                quant(1)
+            else:
+                regroup(0)
+                regroup(1)
+                quant(0)
+                quant(1)
+
 
         banks = {}
         s_t = {}
@@ -193,66 +216,103 @@ def tile_lstmmirrored_pa_kernel(tc, x, hist, Wix, Wih, b_i, Wcx, Wch, b_c, out):
                 in_=st[h][:, 2 * a:2 * a + 2, :],
             )
 
-        def close(nh, gate, h, i):
+        d_t = {}
+        u_t = {}
+
+        def stage1(nh, gate, h, i):
             bank = banks[(h, i)]
             func = ACT.Sigmoid if gate == 0 else ACT.Tanh
-            if gate == 0:
-                s_t[(h, i)] = spool.tile([P, 512], F32, name="s", tag="s")
-                dst = s_t[(h, i)]
-            else:
-                dst = gpool.tile([P, 512], F32, name="gt", tag="gt")
             if FORM[(nh, h)] == "B":
+                if gate == 0:
+                    s_t[(h, i)] = spool.tile([P, 512], F32, name="s", tag="s")
+                    d_t[(h, i)] = s_t[(h, i)]
+                else:
+                    d_t[(h, i)] = gpool.tile([P, 512], F32, name="gt", tag="gt")
                 col = gate * 8 + nh * 4 + i
-                nc.scalar.activation(out=dst[:], in_=bank[:], func=func, bias=bT[:, col:col + 1])
+                nc.scalar.activation(out=d_t[(h, i)][:], in_=bank[:], func=func, bias=bT[:, col:col + 1])
             else:
                 lo = gate * 1024 + nh * 512
-                u = upool.tile([P, 512], F32, name="u", tag="u")
-                nc.vector.tensor_tensor(out=u[:], in0=bank[:], in1=bb[:, lo:lo + 512], op=ALU.add)
-                nc.scalar.activation(out=dst[:], in_=u[:], func=func)
-            if gate == 1:
-                s = s_t[(h, i)]
-                if FORM[(nh, h)] == "B":
-                    nc.vector.tensor_tensor(out=s[:], in0=s[:], in1=dst[:], op=ALU.mult)
+                u_t[(h, i)] = upool.tile([P, 512], F32, name="u", tag="u")
+                nc.vector.tensor_tensor(out=u_t[(h, i)][:], in0=bank[:], in1=bb[:, lo:lo + 512], op=ALU.add)
+
+        def stage2(nh, gate, h, i):
+            func = ACT.Sigmoid if gate == 0 else ACT.Tanh
+            if FORM[(nh, h)] == "B":
+                if gate == 1:
+                    s = s_t[(h, i)]
+                    nc.vector.tensor_tensor(out=s[:], in0=s[:], in1=d_t[(h, i)][:], op=ALU.mult)
+            else:
+                if gate == 0:
+                    s_t[(h, i)] = spool.tile([P, 512], F32, name="s", tag="s")
+                    d_t[(h, i)] = s_t[(h, i)]
                 else:
-                    nc.vector.tensor_tensor(out=st[h][:, i, :], in0=s[:], in1=dst[:], op=ALU.mult)
-                    if i % 2 == 1:
-                        store(nh, h, i // 2)
+                    d_t[(h, i)] = gpool.tile([P, 512], F32, name="gt", tag="gt")
+                nc.scalar.activation(out=d_t[(h, i)][:], in_=u_t[(h, i)][:], func=func)
+
+        def stage3(nh, gate, h, i):
+            if FORM[(nh, h)] == "A" and gate == 1:
+                eng = nc.gpsimd if (h * 4 + i) in G_PROD else nc.vector
+                eng.tensor_tensor(out=st[h][:, i, :], in0=s_t[(h, i)][:], in1=d_t[(h, i)][:], op=ALU.mult)
+                if i % 2 == 1:
+                    store(nh, h, i // 2)
 
         def turn_back(nh, h):
             for tl in range(4):
                 bt = psum.tile([P, 512], F32, name="bt", tag="bank")
                 for i in range(4):
                     nc.tensor.transpose(bt[:, i * P:(i + 1) * P], s_t[(h, i)][:, tl * P:(tl + 1) * P], ident[:])
-                if tl % 2 == 0:
-                    nc.scalar.copy(out=st[h][:, tl, :], in_=bt[:])
-                else:
+                if tl in T_ON_V:
                     nc.vector.tensor_copy(out=st[h][:, tl, :], in_=bt[:])
+                else:
+                    nc.scalar.copy(out=st[h][:, tl, :], in_=bt[:])
+                if tl % 2 == 1:
                     store(nh, h, tl // 2)
 
         groups = [(h, i) for h in range(2) for i in range(4)]
+        items = []
+        for nh in range(2):
+            for gate in range(2):
+                if (nh, gate) in SPLIT:
+                    for part in range(2):
+                        for h, i in groups:
+                            items.append((nh, gate, h, i, (2 * part, 2 * part + 1)))
+                else:
+                    for h, i in groups:
+                        items.append((nh, gate, h, i, (0, 1, 2, 3)))
+        later = {}
+
+        def defer(n, fn, args):
+            later[n] = later.get(n, []) + [(fn, args)]
+
         prep_w(0)
+        x_quant(1, 1)
         prep_w(1)
-        for k in range(8):
-            nh, gate, part = hcs[k]
-            if k + 2 < 8:
-                prep_w(k + 2)
-            if part == 0:
+        n_items = len(items)
+        for n in range(n_items + 8):
+            for k in range(2, 8):
+                if PREP_AT[k] == n:
+                    prep_w(k)
+            if n == 0:
                 for h, i in groups:
                     banks[(h, i)] = psum.tile([P, 512], F32, name="acc", tag="bank")
-            if gate == 1 and part == 1:
-                for h in range(2):
-                    st[h] = stpool.tile([P, 4, 512], F32, name="st", tag="st")
-            if k == 0:
                 for c in range(2):
                     for h, i in groups:
-                        mx(nh, gate, h, i, c)
-            else:
-                for h, i in groups:
-                    for c in (2 * part, 2 * part + 1):
-                        mx(nh, gate, h, i, c)
-                    if part == 1:
-                        close(nh, gate, h, i)
-            if gate == 1 and part == 1:
-                for h in range(2):
-                    if FORM[(nh, h)] == "B":
-                        turn_back(nh, h)
+                        mx(0, 0, h, i, c)
+            elif n < 8:
+                pass
+            elif n < n_items:
+                nh, gate, h, i, cs = items[n]
+                if cs[0] == 0:
+                    banks[(h, i)] = psum.tile([P, 512], F32, name="acc", tag="bank")
+                if gate == 1 and cs[-1] == 3 and i == 0:
+                    st[h] = stpool.tile([P, 4, 512], F32, name="st", tag="st")
+                for c in cs:
+                    mx(nh, gate, h, i, c)
+                if cs[-1] == 3:
+                    stage1(nh, gate, h, i)
+                    defer(n + LAG1, stage2, (nh, gate, h, i))
+                    defer(n + LAG2, stage3, (nh, gate, h, i))
+                    if gate == 1 and i == 3 and FORM[(nh, h)] == "B":
+                        defer(n + LAG1 + TLAG, turn_back, (nh, h))
+            for fn, args in later.get(n, []):
+                fn(*args)

@@ -17,16 +17,16 @@ ALU = mybir.AluOpType
 P = 128
 FLOPS = 2 * 1024 * 2048 * 2048
 
-FORM = {(0, 0): "B", (0, 1): "B", (1, 0): "A", (1, 1): "A"}
-S_REGROUP = ((1, 0), (1, 1), (3, 0), (4, 0), (5, 0), (6, 0))
-V_XCOPY = (1, 3, 5, 7)
+FORM = {(0, 0): 'B', (0, 1): 'B', (1, 0): 'A', (1, 1): 'A'}
+R_AT = {(1, 0): (0, 'S'), (1, 1): (0, 'V'), (2, 0): (2, 'V'), (2, 1): (6, 'S'), (3, 0): (17, 'V'), (3, 1): (6, 'V'), (4, 0): (17, 'S'), (4, 1): (17, 'V'), (5, 0): (21, 'V'), (5, 1): (23, 'S'), (6, 0): (31, 'S'), (6, 1): (33, 'S'), (7, 0): (32, 'V'), (7, 1): (34, 'V')}
+Q_AT = {(1, 0): 0, (1, 1): 0, (2, 0): 3, (2, 1): 6, (3, 0): 18, (3, 1): 11, (4, 0): 24, (4, 1): 19, (5, 0): 24, (5, 1): 25, (6, 0): 32, (6, 1): 37, (7, 0): 32, (7, 1): 37}
+V_XCOPY = (0, 7, 10, 11)
 SPLIT = ((0, 0), (0, 1))
 G_PROD = ()
-PREP_AT = {2: 0, 3: 8, 4: 16, 5: 24, 6: 34, 7: 38}
 LAG1 = 1
 LAG2 = 2
-TLAG = 2
-T_ON_V = (1, 3)
+TLAG = 4
+T_ON_V = (1,)
 PIN = True
 
 
@@ -155,37 +155,27 @@ def tile_lstmmirrored_pa_kernel(tc, x, hist, Wix, Wih, b_i, Wcx, Wch, b_c, out):
         for k in range(4, 8):
             load_w(k)
 
-        def prep_w(k):
-            nh, gate, part = hcs[k]
-            gw = {}
+        gw = {}
+        ready = set()
 
-            def regroup(g):
-                gw[g] = grp.tile([P, 2048], BF16, name="gw%d%d" % (k, g), tag="grp", align_bytes=64)
-                dst = gw[g][:].rearrange("q (c i t) -> q c t i", i=4, t=4)
-                srcv = wraw[k][:, g * 2048:(g + 1) * 2048].rearrange("q (t c i) -> q c t i", t=4, i=4)
-                if (k, g) in S_REGROUP:
-                    nc.scalar.copy(out=dst, in_=srcv)
-                else:
-                    nc.vector.tensor_copy(out=dst, in_=srcv)
-
-            def quant(g):
-                lo = (gate * 4 + part * 2 + g) * 1024 + nh * 512
-                nc.vector.quantize_mx(
-                    out=wq[:, lo:lo + 512].bitcast(FP8X4),
-                    scales=ws[:, lo:lo + 512],
-                    in_=gw[g][:],
-                )
-
-            if k == 0:
-                regroup(0)
-                quant(0)
-                regroup(1)
-                quant(1)
+        def regroup(k, g, eng):
+            gw[(k, g)] = grp.tile([P, 2048], BF16, name="gw%d%d" % (k, g), tag="grp", align_bytes=64)
+            dst = gw[(k, g)][:].rearrange("q (c i t) -> q c t i", i=4, t=4)
+            srcv = wraw[k][:, g * 2048:(g + 1) * 2048].rearrange("q (t c i) -> q c t i", t=4, i=4)
+            if eng == "S":
+                nc.scalar.copy(out=dst, in_=srcv)
             else:
-                regroup(0)
-                regroup(1)
-                quant(0)
-                quant(1)
+                nc.vector.tensor_copy(out=dst, in_=srcv)
+
+        def quant(k, g):
+            nh, gate, part = hcs[k]
+            lo = (gate * 4 + part * 2 + g) * 1024 + nh * 512
+            nc.vector.quantize_mx(
+                out=wq[:, lo:lo + 512].bitcast(FP8X4),
+                scales=ws[:, lo:lo + 512],
+                in_=gw[(k, g)][:],
+            )
+            ready.add((nh, gate, part * 2 + g))
 
 
         banks = {}
@@ -193,6 +183,7 @@ def tile_lstmmirrored_pa_kernel(tc, x, hist, Wix, Wih, b_i, Wcx, Wch, b_c, out):
         st = {}
 
         def mx(nh, gate, h, i, c):
+            assert (nh, gate, c) in ready
             wl = (gate * 4 + c) * 1024 + nh * 512
             if FORM[(nh, h)] == "B":
                 a, b = wl + i * P, c * 1024 + h * 512
@@ -284,22 +275,27 @@ def tile_lstmmirrored_pa_kernel(tc, x, hist, Wix, Wih, b_i, Wcx, Wch, b_c, out):
         def defer(n, fn, args):
             later[n] = later.get(n, []) + [(fn, args)]
 
-        prep_w(0)
+        for g in range(2):
+            regroup(0, g, "V")
+            quant(0, g)
         x_quant(1, 1)
-        prep_w(1)
+        subs = [(k, g) for k in range(1, 8) for g in range(2)]
         n_items = len(items)
         for n in range(n_items + 8):
-            for k in range(2, 8):
-                if PREP_AT[k] == n:
-                    prep_w(k)
-            if n == 0:
-                for h, i in groups:
-                    banks[(h, i)] = psum.tile([P, 512], F32, name="acc", tag="bank")
-                for c in range(2):
+            for kg in subs:
+                if R_AT[kg][0] == n:
+                    regroup(kg[0], kg[1], R_AT[kg][1])
+            for kg in subs:
+                if Q_AT[kg] == n:
+                    quant(kg[0], kg[1])
+            if n < n_items and items[n][4] == (0, 1):
+                nh, gate, h, i, cs = items[n]
+                if (h, i) == (0, 0):
                     for h, i in groups:
-                        mx(0, 0, h, i, c)
-            elif n < 8:
-                pass
+                        banks[(h, i)] = psum.tile([P, 512], F32, name="acc", tag="bank")
+                    for c in range(2):
+                        for h, i in groups:
+                            mx(nh, gate, h, i, c)
             elif n < n_items:
                 nh, gate, h, i, cs = items[n]
                 if cs[0] == 0:

@@ -18,11 +18,12 @@ P = 128
 FLOPS = 2 * 1024 * 2048 * 2048
 
 FORM = {(0, 0): 'B', (0, 1): 'B', (1, 0): 'A', (1, 1): 'A'}
-R_AT = {(1, 0): (0, 'S'), (1, 1): (0, 'V'), (2, 0): (2, 'V'), (2, 1): (6, 'S'), (3, 0): (17, 'V'), (3, 1): (6, 'V'), (4, 0): (17, 'S'), (4, 1): (17, 'V'), (5, 0): (21, 'V'), (5, 1): (23, 'S'), (6, 0): (31, 'S'), (6, 1): (33, 'S'), (7, 0): (32, 'V'), (7, 1): (34, 'V')}
-Q_AT = {(1, 0): 0, (1, 1): 0, (2, 0): 3, (2, 1): 6, (3, 0): 18, (3, 1): 11, (4, 0): 24, (4, 1): 19, (5, 0): 24, (5, 1): 25, (6, 0): 32, (6, 1): 37, (7, 0): 32, (7, 1): 37}
-V_XCOPY = (0, 7, 10, 11)
+R_AT = {(1, 0): (0, 'S'), (1, 1): (0, 'VS'), (2, 0): (4, 'VS'), (2, 1): (4, 'VS'), (3, 0): (16, 'VS'), (3, 1): (9, 'V'), (4, 0): (17, 'VS'), (4, 1): (16, 'VS'), (5, 0): (23, 'V'), (5, 1): (18, 'S'), (6, 0): (34, 'S'), (6, 1): (34, 'S'), (7, 0): (34, 'V'), (7, 1): (35, 'V')}
+Q_AT = {(1, 0): 0, (1, 1): 0, (2, 0): 7, (2, 1): 9, (3, 0): 18, (3, 1): 15, (4, 0): 23, (4, 1): 20, (5, 0): 23, (5, 1): 25, (6, 0): 35, (6, 1): 37, (7, 0): 36, (7, 1): 37}
+V_XCOPY = (1, 2, 3, 8, 10)
 SPLIT = ((0, 0), (0, 1))
-G_PROD = ()
+G_PROD = (0, 2, 3, 5)
+SINGLE = (1, 2, 3)
 LAG1 = 1
 LAG2 = 2
 TLAG = 4
@@ -158,24 +159,27 @@ def tile_lstmmirrored_pa_kernel(tc, x, hist, Wix, Wih, b_i, Wcx, Wch, b_c, out):
         gw = {}
         ready = set()
 
-        def regroup(k, g, eng):
-            gw[(k, g)] = grp.tile([P, 2048], BF16, name="gw%d%d" % (k, g), tag="grp", align_bytes=64)
-            dst = gw[(k, g)][:].rearrange("q (c i t) -> q c t i", i=4, t=4)
-            srcv = wraw[k][:, g * 2048:(g + 1) * 2048].rearrange("q (t c i) -> q c t i", t=4, i=4)
+        def regroup(k, g, eng, lo=0, cols=512):
+            if lo == 0:
+                gw[(k, g)] = grp.tile([P, 2048], BF16, name="gw%d%d" % (k, g), tag="grp", align_bytes=64)
+            dst = gw[(k, g)][:, 4 * lo:4 * (lo + cols)].rearrange("q (c i t) -> q c t i", i=4, t=4)
+            srcv = wraw[k][:, g * 2048:(g + 1) * 2048].rearrange("q (t n) -> q t n", t=4)
+            srcv = srcv[:, :, lo:lo + cols].rearrange("q t (c i) -> q c t i", i=4)
             if eng == "S":
                 nc.scalar.copy(out=dst, in_=srcv)
             else:
                 nc.vector.tensor_copy(out=dst, in_=srcv)
 
-        def quant(k, g):
+        def quant(k, g, c0=0, cols=512):
             nh, gate, part = hcs[k]
-            lo = (gate * 4 + part * 2 + g) * 1024 + nh * 512
+            lo = (gate * 4 + part * 2 + g) * 1024 + nh * 512 + c0
             nc.vector.quantize_mx(
-                out=wq[:, lo:lo + 512].bitcast(FP8X4),
-                scales=ws[:, lo:lo + 512],
-                in_=gw[(k, g)][:],
+                out=wq[:, lo:lo + cols].bitcast(FP8X4),
+                scales=ws[:, lo:lo + cols],
+                in_=gw[(k, g)][:, 4 * c0:4 * (c0 + cols)],
             )
-            ready.add((nh, gate, part * 2 + g))
+            for j in range(c0 // P, (c0 + cols) // P):
+                ready.add((nh, gate, part * 2 + g, j))
 
 
         banks = {}
@@ -183,7 +187,8 @@ def tile_lstmmirrored_pa_kernel(tc, x, hist, Wix, Wih, b_i, Wcx, Wch, b_c, out):
         st = {}
 
         def mx(nh, gate, h, i, c):
-            assert (nh, gate, c) in ready
+            for j in ((i,) if FORM[(nh, h)] == "B" else range(4)):
+                assert (nh, gate, c, j) in ready
             wl = (gate * 4 + c) * 1024 + nh * 512
             if FORM[(nh, h)] == "B":
                 a, b = wl + i * P, c * 1024 + h * 512
@@ -201,10 +206,10 @@ def tile_lstmmirrored_pa_kernel(tc, x, hist, Wix, Wih, b_i, Wcx, Wch, b_c, out):
                 stop=(c == 3),
             )
 
-        def store(nh, h, a):
+        def store(nh, h, lo, cnt):
             nc.sync.dma_start(
-                out=ov[:, h * 4 + 2 * a:h * 4 + 2 * a + 2, nh * 512:(nh + 1) * 512],
-                in_=st[h][:, 2 * a:2 * a + 2, :],
+                out=ov[:, h * 4 + lo:h * 4 + lo + cnt, nh * 512:(nh + 1) * 512],
+                in_=st[h][:, lo:lo + cnt, :],
             )
 
         d_t = {}
@@ -244,8 +249,10 @@ def tile_lstmmirrored_pa_kernel(tc, x, hist, Wix, Wih, b_i, Wcx, Wch, b_c, out):
             if FORM[(nh, h)] == "A" and gate == 1:
                 eng = nc.gpsimd if (h * 4 + i) in G_PROD else nc.vector
                 eng.tensor_tensor(out=st[h][:, i, :], in0=s_t[(h, i)][:], in1=d_t[(h, i)][:], op=ALU.mult)
-                if i % 2 == 1:
-                    store(nh, h, i // 2)
+                if (h * 4 + i) // 2 in SINGLE:
+                    store(nh, h, i, 1)
+                elif i % 2 == 1:
+                    store(nh, h, i - 1, 2)
 
         def turn_back(nh, h):
             for tl in range(4):
@@ -257,7 +264,7 @@ def tile_lstmmirrored_pa_kernel(tc, x, hist, Wix, Wih, b_i, Wcx, Wch, b_c, out):
                 else:
                     nc.scalar.copy(out=st[h][:, tl, :], in_=bt[:])
                 if tl % 2 == 1:
-                    store(nh, h, tl // 2)
+                    store(nh, h, tl - 1, 2)
 
         groups = [(h, i) for h in range(2) for i in range(4)]
         items = []
@@ -276,15 +283,20 @@ def tile_lstmmirrored_pa_kernel(tc, x, hist, Wix, Wih, b_i, Wcx, Wch, b_c, out):
             later[n] = later.get(n, []) + [(fn, args)]
 
         for g in range(2):
-            regroup(0, g, "V")
-            quant(0, g)
+            for lo in (0, 256):
+                regroup(0, g, "V", lo, 256)
+                quant(0, g, lo, 256)
         x_quant(1, 1)
         subs = [(k, g) for k in range(1, 8) for g in range(2)]
         n_items = len(items)
         for n in range(n_items + 8):
             for kg in subs:
                 if R_AT[kg][0] == n:
-                    regroup(kg[0], kg[1], R_AT[kg][1])
+                    if R_AT[kg][1] == "VS":
+                        regroup(kg[0], kg[1], "V", 0, 336)
+                        regroup(kg[0], kg[1], "S", 336, 176)
+                    else:
+                        regroup(kg[0], kg[1], R_AT[kg][1])
             for kg in subs:
                 if Q_AT[kg] == n:
                     quant(kg[0], kg[1])
@@ -294,7 +306,7 @@ def tile_lstmmirrored_pa_kernel(tc, x, hist, Wix, Wih, b_i, Wcx, Wch, b_c, out):
                     for h, i in groups:
                         banks[(h, i)] = psum.tile([P, 512], F32, name="acc", tag="bank")
                     for c in range(2):
-                        for h, i in groups:
+                        for h, i in sorted(groups, key=lambda hi: hi[1] // 2):
                             mx(nh, gate, h, i, c)
             elif n < n_items:
                 nh, gate, h, i, cs = items[n]

@@ -18,14 +18,15 @@ P = 128
 FLOPS = 2 * 1024 * 2048 * 2048
 
 FORM = {(0, 0): 'B', (0, 1): 'B', (1, 0): 'A', (1, 1): 'A'}
-R_AT = {(1, 0): (0, 'S'), (1, 1): (0, 'VS'), (2, 0): (4, 'VS'), (2, 1): (4, 'VS'), (3, 0): (16, 'VS'), (3, 1): (9, 'V'), (4, 0): (17, 'VS'), (4, 1): (16, 'VS'), (5, 0): (23, 'V'), (5, 1): (18, 'S'), (6, 0): (34, 'S'), (6, 1): (34, 'S'), (7, 0): (34, 'V'), (7, 1): (35, 'V')}
-Q_AT = {(1, 0): 0, (1, 1): 0, (2, 0): 7, (2, 1): 9, (3, 0): 18, (3, 1): 15, (4, 0): 23, (4, 1): 20, (5, 0): 23, (5, 1): 25, (6, 0): 35, (6, 1): 37, (7, 0): 36, (7, 1): 37}
-V_XCOPY = (1, 2, 3, 8, 10)
+R_AT = {(1, 0): (0, 'S'), (1, 1): (0, 'VS'), (2, 0): (4, 'V'), (2, 1): (4, 'VS'), (3, 0): (17, 'VS'), (3, 1): (13, 'V'), (4, 0): (17, 'VS'), (4, 1): (18, 'VS'), (5, 0): (23, 'V'), (5, 1): (18, 'S'), (6, 0): (32, 'S'), (6, 1): (33, 'S'), (7, 0): (33, 'V'), (7, 1): (30, 'V')}
+Q_AT = {(1, 0): 0, (1, 1): 1, (2, 0): 4, (2, 1): 14, (3, 0): 18, (3, 1): 16, (4, 0): 21, (4, 1): 23, (5, 0): 25, (5, 1): 25, (6, 0): 36, (6, 1): 36, (7, 0): 35, (7, 1): 35}
+V_XCOPY = (3, 4, 7, 10)
 SPLIT = ((0, 0), (0, 1))
-G_PROD = (0, 2, 3, 5)
-SINGLE = (1, 2, 3)
+G_PROD = (8, 9, 10, 11, 12)
+SINGLE = (4, 5, 6, 7)
+TAPER = 2
 LAG1 = 1
-LAG2 = 2
+LAG2 = 3
 TLAG = 4
 T_ON_V = (1,)
 PIN = True
@@ -41,8 +42,8 @@ def tile_lstmmirrored_pa_kernel(tc, x, hist, Wix, Wih, b_i, Wcx, Wch, b_c, out):
         raw = ctx.enter_context(tc.tile_pool(name="raw", bufs=8))
         grp = ctx.enter_context(tc.tile_pool(name="grp", bufs=8))
         spool = ctx.enter_context(tc.tile_pool(name="spool", bufs=12))
-        gpool = ctx.enter_context(tc.tile_pool(name="gpool", bufs=3))
-        upool = ctx.enter_context(tc.tile_pool(name="upool", bufs=3))
+        gpool = ctx.enter_context(tc.tile_pool(name="gpool", bufs=5))
+        upool = ctx.enter_context(tc.tile_pool(name="upool", bufs=4))
         stpool = ctx.enter_context(tc.tile_pool(name="stpool", bufs=2))
         psum = ctx.enter_context(tc.psum_pool(name="psum", bufs=8))
 
@@ -186,7 +187,7 @@ def tile_lstmmirrored_pa_kernel(tc, x, hist, Wix, Wih, b_i, Wcx, Wch, b_c, out):
         s_t = {}
         st = {}
 
-        def mx(nh, gate, h, i, c):
+        def mx(nh, gate, h, i, c, c0=0, cw=512):
             for j in ((i,) if FORM[(nh, h)] == "B" else range(4)):
                 assert (nh, gate, c, j) in ready
             wl = (gate * 4 + c) * 1024 + nh * 512
@@ -194,62 +195,65 @@ def tile_lstmmirrored_pa_kernel(tc, x, hist, Wix, Wih, b_i, Wcx, Wch, b_c, out):
                 a, b = wl + i * P, c * 1024 + h * 512
                 l_c, l_s, r_c, r_s = wq, ws, xq, xs
             else:
-                a, b = c * 1024 + (h * 4 + i) * P, wl
+                a, b = c * 1024 + (h * 4 + i) * P, wl + c0
                 l_c, l_s, r_c, r_s = xq, xs, wq, ws
             nc.tensor.matmul_mx(
-                out=banks[(h, i)][:],
+                out=banks[(h, i, c0)][:, 0:cw],
                 lhsT=l_c[:, a:a + P].bitcast(FP8X4),
                 lhsT_scale=l_s[:, a:a + P],
-                rhs=r_c[:, b:b + 512].bitcast(FP8X4),
-                rhs_scale=r_s[:, b:b + 512],
+                rhs=r_c[:, b:b + cw].bitcast(FP8X4),
+                rhs_scale=r_s[:, b:b + cw],
                 start=(c == 0),
                 stop=(c == 3),
             )
 
-        def store(nh, h, lo, cnt):
+        def store(nh, h, lo, cnt, c0=0, cw=512):
             nc.sync.dma_start(
-                out=ov[:, h * 4 + lo:h * 4 + lo + cnt, nh * 512:(nh + 1) * 512],
-                in_=st[h][:, lo:lo + cnt, :],
+                out=ov[:, h * 4 + lo:h * 4 + lo + cnt, nh * 512 + c0:nh * 512 + c0 + cw],
+                in_=st[h][:, lo:lo + cnt, c0:c0 + cw],
             )
 
         d_t = {}
         u_t = {}
 
-        def stage1(nh, gate, h, i):
-            bank = banks[(h, i)]
+        def stage1(nh, gate, h, i, c0=0, cw=512):
+            bank = banks[(h, i, c0)]
             func = ACT.Sigmoid if gate == 0 else ACT.Tanh
             if FORM[(nh, h)] == "B":
                 if gate == 0:
                     s_t[(h, i)] = spool.tile([P, 512], F32, name="s", tag="s")
-                    d_t[(h, i)] = s_t[(h, i)]
+                    d_t[(h, i, c0)] = s_t[(h, i)]
                 else:
-                    d_t[(h, i)] = gpool.tile([P, 512], F32, name="gt", tag="gt")
+                    d_t[(h, i, c0)] = gpool.tile([P, 512], F32, name="gt", tag="gt")
                 col = gate * 8 + nh * 4 + i
-                nc.scalar.activation(out=d_t[(h, i)][:], in_=bank[:], func=func, bias=bT[:, col:col + 1])
+                nc.scalar.activation(out=d_t[(h, i, c0)][:], in_=bank[:], func=func, bias=bT[:, col:col + 1])
             else:
-                lo = gate * 1024 + nh * 512
-                u_t[(h, i)] = upool.tile([P, 512], F32, name="u", tag="u")
-                nc.vector.tensor_tensor(out=u_t[(h, i)][:], in0=bank[:], in1=bb[:, lo:lo + 512], op=ALU.add)
+                lo = gate * 1024 + nh * 512 + c0
+                u_t[(h, i, c0)] = upool.tile([P, 512], F32, name="u", tag="u")
+                nc.vector.tensor_tensor(out=u_t[(h, i, c0)][:, 0:cw], in0=bank[:, 0:cw], in1=bb[:, lo:lo + cw], op=ALU.add)
 
-        def stage2(nh, gate, h, i):
+        def stage2(nh, gate, h, i, c0=0, cw=512):
             func = ACT.Sigmoid if gate == 0 else ACT.Tanh
             if FORM[(nh, h)] == "B":
                 if gate == 1:
                     s = s_t[(h, i)]
-                    nc.vector.tensor_tensor(out=s[:], in0=s[:], in1=d_t[(h, i)][:], op=ALU.mult)
+                    nc.vector.tensor_tensor(out=s[:], in0=s[:], in1=d_t[(h, i, c0)][:], op=ALU.mult)
             else:
                 if gate == 0:
                     s_t[(h, i)] = spool.tile([P, 512], F32, name="s", tag="s")
-                    d_t[(h, i)] = s_t[(h, i)]
+                    d_t[(h, i, c0)] = s_t[(h, i)]
                 else:
-                    d_t[(h, i)] = gpool.tile([P, 512], F32, name="gt", tag="gt")
-                nc.scalar.activation(out=d_t[(h, i)][:], in_=u_t[(h, i)][:], func=func)
+                    d_t[(h, i, c0)] = gpool.tile([P, 512], F32, name="gt", tag="gt")
+                nc.scalar.activation(out=d_t[(h, i, c0)][:, 0:cw], in_=u_t[(h, i, c0)][:, 0:cw], func=func)
 
-        def stage3(nh, gate, h, i):
+        def stage3(nh, gate, h, i, c0=0, cw=512):
             if FORM[(nh, h)] == "A" and gate == 1:
-                eng = nc.gpsimd if (h * 4 + i) in G_PROD else nc.vector
-                eng.tensor_tensor(out=st[h][:, i, :], in0=s_t[(h, i)][:], in1=d_t[(h, i)][:], op=ALU.mult)
-                if (h * 4 + i) // 2 in SINGLE:
+                eng = nc.gpsimd if (nh * 8 + h * 4 + i) in G_PROD else nc.vector
+                eng.tensor_tensor(out=st[h][:, i, c0:c0 + cw], in0=s_t[(h, i)][:, c0:c0 + cw],
+                                  in1=d_t[(h, i, c0)][:, 0:cw], op=ALU.mult)
+                if cw < 512:
+                    store(nh, h, i, 1, c0, cw)
+                elif (nh * 8 + h * 4 + i) // 2 in SINGLE:
                     store(nh, h, i, 1)
                 elif i % 2 == 1:
                     store(nh, h, i - 1, 2)
@@ -273,10 +277,14 @@ def tile_lstmmirrored_pa_kernel(tc, x, hist, Wix, Wih, b_i, Wcx, Wch, b_c, out):
                 if (nh, gate) in SPLIT:
                     for part in range(2):
                         for h, i in groups:
-                            items.append((nh, gate, h, i, (2 * part, 2 * part + 1)))
+                            items.append((nh, gate, h, i, (2 * part, 2 * part + 1), 0, 512))
                 else:
                     for h, i in groups:
-                        items.append((nh, gate, h, i, (0, 1, 2, 3)))
+                        if (nh, gate) == (1, 1) and h * 4 + i >= 8 - TAPER:
+                            items.append((nh, gate, h, i, (0, 1, 2, 3), 0, 256))
+                            items.append((nh, gate, h, i, (0, 1, 2, 3), 256, 256))
+                        else:
+                            items.append((nh, gate, h, i, (0, 1, 2, 3), 0, 512))
         later = {}
 
         def defer(n, fn, args):
@@ -301,25 +309,25 @@ def tile_lstmmirrored_pa_kernel(tc, x, hist, Wix, Wih, b_i, Wcx, Wch, b_c, out):
                 if Q_AT[kg] == n:
                     quant(kg[0], kg[1])
             if n < n_items and items[n][4] == (0, 1):
-                nh, gate, h, i, cs = items[n]
+                nh, gate, h, i, cs, c0, cw = items[n]
                 if (h, i) == (0, 0):
                     for h, i in groups:
-                        banks[(h, i)] = psum.tile([P, 512], F32, name="acc", tag="bank")
+                        banks[(h, i, 0)] = psum.tile([P, 512], F32, name="acc", tag="bank")
                     for c in range(2):
                         for h, i in sorted(groups, key=lambda hi: hi[1] // 2):
                             mx(nh, gate, h, i, c)
             elif n < n_items:
-                nh, gate, h, i, cs = items[n]
+                nh, gate, h, i, cs, c0, cw = items[n]
                 if cs[0] == 0:
-                    banks[(h, i)] = psum.tile([P, 512], F32, name="acc", tag="bank")
+                    banks[(h, i, c0)] = psum.tile([P, 512], F32, name="acc", tag="bank")
                 if gate == 1 and cs[-1] == 3 and i == 0:
                     st[h] = stpool.tile([P, 4, 512], F32, name="st", tag="st")
                 for c in cs:
-                    mx(nh, gate, h, i, c)
+                    mx(nh, gate, h, i, c, c0, cw)
                 if cs[-1] == 3:
-                    stage1(nh, gate, h, i)
-                    defer(n + LAG1, stage2, (nh, gate, h, i))
-                    defer(n + LAG2, stage3, (nh, gate, h, i))
+                    stage1(nh, gate, h, i, c0, cw)
+                    defer(n + LAG1, stage2, (nh, gate, h, i, c0, cw))
+                    defer(n + LAG2, stage3, (nh, gate, h, i, c0, cw))
                     if gate == 1 and i == 3 and FORM[(nh, h)] == "B":
                         defer(n + LAG1 + TLAG, turn_back, (nh, h))
             for fn, args in later.get(n, []):

@@ -1,8 +1,6 @@
 from contextlib import ExitStack
 
-import concourse.bass as bass
 import concourse.mybir as mybir
-import concourse.tile as tile
 from concourse.masks import make_identity
 
 F32 = mybir.dt.float32
@@ -15,28 +13,32 @@ ACT = mybir.ActivationFunctionType
 ALU = mybir.AluOpType
 
 P = 128
+BANK = 512
 FLOPS = 2 * 1024 * 2048 * 2048
 
-FORM = {(0, 0): 'B', (0, 1): 'B', (1, 0): 'A', (1, 1): 'A'}
-R_AT = {(1, 0): (0, 'S'), (1, 1): (0, 'VS'), (2, 0): (4, 'V'), (2, 1): (4, 'VS'), (3, 0): (17, 'VS'), (3, 1): (13, 'V'), (4, 0): (17, 'VS'), (4, 1): (18, 'VS'), (5, 0): (23, 'V'), (5, 1): (18, 'S'), (6, 0): (32, 'S'), (6, 1): (33, 'S'), (7, 0): (33, 'V'), (7, 1): (30, 'V')}
-Q_AT = {(1, 0): 0, (1, 1): 1, (2, 0): 4, (2, 1): 14, (3, 0): 18, (3, 1): 16, (4, 0): 21, (4, 1): 23, (5, 0): 25, (5, 1): 25, (6, 0): 36, (6, 1): 36, (7, 0): 35, (7, 1): 35}
-V_XCOPY = (3, 4, 7, 10)
-SPLIT = ((0, 0), (0, 1))
-G_PROD = (8, 9, 10, 11, 12)
-SINGLE = (4, 5, 6, 7)
-TAPER = 2
-LAG1 = 1
-LAG2 = 3
-TLAG = 4
-T_ON_V = (1,)
-PIN = True
+REGROUP_AT = {
+    (1, 0): (0, "S"), (1, 1): (0, "VS"), (2, 0): (4, "V"), (2, 1): (4, "VS"), (3, 0): (17, "VS"), (3, 1): (13, "V"),
+    (4, 0): (17, "VS"), (4, 1): (18, "VS"), (5, 0): (23, "V"), (5, 1): (18, "S"), (6, 0): (32, "S"), (6, 1): (33, "S"),
+    (7, 0): (33, "V"), (7, 1): (30, "V"),
+}
+QUANT_AT = {
+    (1, 0): 0, (1, 1): 1, (2, 0): 4, (2, 1): 14, (3, 0): 18, (3, 1): 16, (4, 0): 21, (4, 1): 23, (5, 0): 25, (5, 1): 25,
+    (6, 0): 36, (6, 1): 36, (7, 0): 35, (7, 1): 35,
+}
+VECTOR_SHARE = 336
+VECTOR_X_BANKS = (3, 4, 7, 10)
+STEP_2_LAG = 1
+STEP_3_LAG = 3
+TURN_BACK_LAG = 5
+VECTOR_BACK_BANK = 1
+GPSIMD_PRODUCTS = 5
+HALVED_GROUPS = 2
 
 
 def tile_lstmmirrored_pa_kernel(tc, x, hist, Wix, Wih, b_i, Wcx, Wch, b_c, out):
     nc = tc.nc
     with ExitStack() as ctx:
-        if PIN:
-            ctx.enter_context(tc.manual_schedule())
+        ctx.enter_context(tc.manual_schedule())
         const = ctx.enter_context(tc.tile_pool(name="const", bufs=1))
         keep = ctx.enter_context(tc.tile_pool(name="keep", bufs=1))
         raw = ctx.enter_context(tc.tile_pool(name="raw", bufs=8))
@@ -47,288 +49,271 @@ def tile_lstmmirrored_pa_kernel(tc, x, hist, Wix, Wih, b_i, Wcx, Wch, b_c, out):
         stpool = ctx.enter_context(tc.tile_pool(name="stpool", bufs=2))
         psum = ctx.enter_context(tc.psum_pool(name="psum", bufs=8))
 
-        xv = x.rearrange("(p t) k -> p (t k)", t=8)
-        hv = hist.rearrange("(p t) k -> p (t k)", t=8)
-        ov = out.rearrange("(p t) n -> p t n", t=8)
-        mats = ((Wix, Wih), (Wcx, Wch))
-        hcs = [(nh, gate, part) for nh in range(2) for gate in range(2) for part in range(2)]
+        x_rows = x.rearrange("(p t) k -> p (t k)", t=8)
+        hist_rows = hist.rearrange("(p t) k -> p (t k)", t=8)
+        out_rows = out.rearrange("(p t) n -> p t n", t=8)
+        matrices = ((Wix, Wih), (Wcx, Wch))
+        blocks = [(nh, gate, part) for nh in range(2) for gate in range(2) for part in range(2)]
 
         warm = const.tile([P, 1], F32, name="warm")
         nc.vector.memset(warm[:], 0.0)
         nc.scalar.activation(out=warm[:], in_=warm[:], func=ACT.Sigmoid)
         ident = const.tile([P, P], F32, name="ident")
         make_identity(nc, ident[:])
-        zrow = const.tile([P, 2048], BF16, name="zrow")
-        nc.vector.memset(zrow[:].bitcast(I32), 0)
-        nc.scalar.dma_start(out=zrow[0:1, 0:1024], in_=b_i.rearrange("(o n) -> o n", o=1))
-        nc.scalar.dma_start(out=zrow[0:1, 1024:2048], in_=b_c.rearrange("(o n) -> o n", o=1))
+        bias_row = const.tile([P, 2048], BF16, name="bias_row")
+        nc.vector.memset(bias_row[:].bitcast(I32), 0)
+        nc.scalar.dma_start(out=bias_row[0:1, 0:1024], in_=b_i.rearrange("(o n) -> o n", o=1))
+        nc.scalar.dma_start(out=bias_row[0:1, 1024:2048], in_=b_c.rearrange("(o n) -> o n", o=1))
         ones = const.tile([P, P], BF16, name="ones")
         nc.vector.memset(ones[:], 1.0)
+        bias_col = const.tile([P, 8], F32, name="bias_col")
+        bias_wide = const.tile([P, 2 * BANK], F32, name="bias_wide")
 
-        xq = keep.tile([P, 4 * 1024], U32, name="xq", align_bytes=64)
-        xs = keep.tile([P, 4 * 1024], U8, name="xs", align_bytes=64)
-        wq = keep.tile([P, 8 * 1024], U32, name="wq", align_bytes=64)
-        ws = keep.tile([P, 8 * 1024], U8, name="ws", align_bytes=64)
+        x_codes = keep.tile([P, 4 * 1024], U32, name="x_codes", align_bytes=64)
+        x_scales = keep.tile([P, 4 * 1024], U8, name="x_scales", align_bytes=64)
+        w_codes = keep.tile([P, 8 * 1024], U32, name="w_codes", align_bytes=64)
+        w_scales = keep.tile([P, 8 * 1024], U8, name="w_scales", align_bytes=64)
 
-        xraw = []
-        for si, v in enumerate((xv, hv)):
-            for hh in range(2):
-                r = raw.tile([P, 4096], BF16, name="xr%d%d" % (si, hh), tag="raw")
+        x_raw = []
+        for si, rows in enumerate((x_rows, hist_rows)):
+            for h in range(2):
+                tile4 = raw.tile([P, 4096], BF16, name="x_raw%d%d" % (si, h), tag="raw")
                 for a in range(2):
-                    lo = (hh * 4 + a * 2) * 1024
-                    nc.sync.dma_start(out=r[:, a * 2048:(a + 1) * 2048], in_=v[:, lo:lo + 2048])
-                xraw.append(r)
+                    lo = (h * 4 + a * 2) * 1024
+                    nc.sync.dma_start(out=tile4[:, a * 2048:(a + 1) * 2048], in_=rows[:, lo:lo + 2048])
+                x_raw.append(tile4)
 
-        wraw = {}
+        w_raw = {}
 
-        def load_w(k):
-            nh, gate, part = hcs[k]
-            wv = mats[gate][part][:, nh * 512:(nh + 1) * 512].rearrange("(a q e) c -> q a e c", a=4, e=2)
-            r = raw.tile([P, 4096], BF16, name="wr%d" % k, tag="raw")
-            rv = r[:].rearrange("q (a e c) -> q a e c", a=4, e=2)
+        def load_weights(k):
+            nh, gate, part = blocks[k]
+            src = matrices[gate][part][:, nh * BANK:(nh + 1) * BANK].rearrange("(a q e) c -> q a e c", a=4, e=2)
+            w_raw[k] = raw.tile([P, 4096], BF16, name="w_raw%d" % k, tag="raw")
+            dst = w_raw[k][:].rearrange("q (a e c) -> q a e c", a=4, e=2)
             if k < 2:
                 for a in range(4):
-                    nc.sync.dma_start(out=rv[:, a, :, :], in_=wv[:, a, :, :])
+                    nc.sync.dma_start(out=dst[:, a, :, :], in_=src[:, a, :, :])
             else:
                 for e in range(2):
-                    nc.sync.dma_start(out=rv[:, :, e, :], in_=wv[:, :, e, :])
-            wraw[k] = r
+                    nc.sync.dma_start(out=dst[:, :, e, :], in_=src[:, :, e, :])
 
         for k in range(4):
-            load_w(k)
+            load_weights(k)
 
-        gx = {}
+        x_grouped = {}
 
-        def x_block(si, tp):
-            rf = xraw[si * 2 + tp // 2][:].bitcast(F32)
+        def transpose_pair(si, tp):
+            words = x_raw[si * 2 + tp // 2][:].bitcast(F32)
             h = tp // 2
             for g in range(2):
-                bk = psum.tile([P, 512], F32, name="bkx", tag="bank")
+                bank = psum.tile([P, BANK], F32, name="bank_x", tag="bank")
                 for u in range(2):
                     for t2 in range(2):
                         w0 = ((tp % 2) * 2 + t2) * 512 + (2 * g + u) * P
                         o0 = (u * 2 + t2) * P
-                        nc.tensor.transpose(bk[:, o0:o0 + P], rf[:, w0:w0 + P], ident[:])
+                        nc.tensor.transpose(bank[:, o0:o0 + P], words[:, w0:w0 + P], ident[:])
                 c = 2 * si + g
                 if tp % 2 == 0:
-                    gx[(c, h)] = grp.tile([P, 2048], BF16, name="gx%d%d" % (c, h), tag="grp", align_bytes=64)
-                dst = gx[(c, h)][:].bitcast(F32).rearrange("q (c u) -> q c u", u=2)
+                    x_grouped[(c, h)] = grp.tile([P, 2048], BF16, name="x_grouped%d%d" % (c, h), tag="grp", align_bytes=64)
+                dst = x_grouped[(c, h)][:].bitcast(F32).rearrange("q (c u) -> q c u", u=2)
                 dst = dst[:, (tp % 2) * 256:(tp % 2) * 256 + 256, :]
-                srcv = bk[:].rearrange("q (u c) -> q c u", u=2)
-                if (si * 8 + tp * 2 + g) in V_XCOPY:
-                    nc.vector.tensor_copy(out=dst, in_=srcv)
+                src = bank[:].rearrange("q (u c) -> q c u", u=2)
+                if (si * 8 + tp * 2 + g) in VECTOR_X_BANKS:
+                    nc.vector.tensor_copy(out=dst, in_=src)
                 else:
-                    nc.scalar.copy(out=dst, in_=srcv)
+                    nc.scalar.copy(out=dst, in_=src)
 
-        def x_quant(si, h):
+        def quantise_x(si, h):
             for g in range(2):
                 c = 2 * si + g
-                lo = c * 1024 + h * 512
+                lo = c * 1024 + h * BANK
                 nc.vector.quantize_mx(
-                    out=xq[:, lo:lo + 512].bitcast(FP8X4),
-                    scales=xs[:, lo:lo + 512],
-                    in_=gx[(c, h)][:],
+                    out=x_codes[:, lo:lo + BANK].bitcast(FP8X4),
+                    scales=x_scales[:, lo:lo + BANK],
+                    in_=x_grouped[(c, h)][:],
                 )
-
-        def bias_prep():
-            bkb = psum.tile([P, 512], F32, name="bkb", tag="bank")
-            for col in range(16):
-                nc.tensor.matmul(bkb[:, col * 32:(col + 1) * 32], lhsT=zrow[:, col * P:(col + 1) * P], rhs=ones[:, 0:32],
-                                 start=True, stop=True)
-            nc.scalar.copy(out=bT[:], in_=bkb[:].rearrange("p (c r) -> p c r", r=32)[:, :, 0])
-            for gate in range(2):
-                for nh in range(2):
-                    if "A" in (FORM[(nh, 0)], FORM[(nh, 1)]):
-                        lo = gate * 1024 + nh * 512
-                        bko = psum.tile([P, 512], F32, name="bko", tag="bank")
-                        nc.tensor.matmul(bko[:], lhsT=ones[:], rhs=zrow[:, lo:lo + 512], start=True, stop=True)
-                        nc.scalar.copy(out=bb[:, lo:lo + 512], in_=bko[:])
-
-        bT = const.tile([P, 16], F32, name="bT")
-        bb = const.tile([P, 2048], F32, name="bb")
 
         for si in range(2):
             for tp in range(4):
-                x_block(si, tp)
+                transpose_pair(si, tp)
                 if (si, tp) in ((0, 2), (1, 0), (1, 2)):
-                    x_quant((si * 4 + tp - 2) // 4, ((si * 4 + tp - 2) % 4) // 2)
+                    done = si * 4 + tp - 2
+                    quantise_x(done // 4, (done % 4) // 2)
 
-        bias_prep()
+        bank = psum.tile([P, BANK], F32, name="bank_b", tag="bank")
+        for col in range(8):
+            lo = (col // 4) * 1024 + (col % 4) * P
+            nc.tensor.matmul(bank[:, col * 32:(col + 1) * 32], lhsT=bias_row[:, lo:lo + P], rhs=ones[:, 0:32],
+                             start=True, stop=True)
+        nc.scalar.copy(out=bias_col[:], in_=bank[:, 0:256].rearrange("p (c r) -> p c r", r=32)[:, :, 0])
+        for gate in range(2):
+            bank = psum.tile([P, BANK], F32, name="bank_w", tag="bank")
+            lo = gate * 1024 + BANK
+            nc.tensor.matmul(bank[:], lhsT=ones[:], rhs=bias_row[:, lo:lo + BANK], start=True, stop=True)
+            nc.scalar.copy(out=bias_wide[:, gate * BANK:(gate + 1) * BANK], in_=bank[:])
+
         for k in range(4, 8):
-            load_w(k)
+            load_weights(k)
 
-        gw = {}
-        ready = set()
+        w_grouped = {}
 
-        def regroup(k, g, eng, lo=0, cols=512):
+        def regroup(k, g, engine, lo=0, cols=BANK):
             if lo == 0:
-                gw[(k, g)] = grp.tile([P, 2048], BF16, name="gw%d%d" % (k, g), tag="grp", align_bytes=64)
-            dst = gw[(k, g)][:, 4 * lo:4 * (lo + cols)].rearrange("q (c i t) -> q c t i", i=4, t=4)
-            srcv = wraw[k][:, g * 2048:(g + 1) * 2048].rearrange("q (t n) -> q t n", t=4)
-            srcv = srcv[:, :, lo:lo + cols].rearrange("q t (c i) -> q c t i", i=4)
-            if eng == "S":
-                nc.scalar.copy(out=dst, in_=srcv)
+                w_grouped[(k, g)] = grp.tile([P, 2048], BF16, name="w_grouped%d%d" % (k, g), tag="grp", align_bytes=64)
+            dst = w_grouped[(k, g)][:, 4 * lo:4 * (lo + cols)].rearrange("q (c i t) -> q c t i", i=4, t=4)
+            src = w_raw[k][:, g * 2048:(g + 1) * 2048].rearrange("q (t n) -> q t n", t=4)
+            src = src[:, :, lo:lo + cols].rearrange("q t (c i) -> q c t i", i=4)
+            if engine == "S":
+                nc.scalar.copy(out=dst, in_=src)
             else:
-                nc.vector.tensor_copy(out=dst, in_=srcv)
+                nc.vector.tensor_copy(out=dst, in_=src)
 
-        def quant(k, g, c0=0, cols=512):
-            nh, gate, part = hcs[k]
-            lo = (gate * 4 + part * 2 + g) * 1024 + nh * 512 + c0
+        def quantise_w(k, g, lo=0, cols=BANK):
+            nh, gate, part = blocks[k]
+            at = (gate * 4 + part * 2 + g) * 1024 + nh * BANK + lo
             nc.vector.quantize_mx(
-                out=wq[:, lo:lo + cols].bitcast(FP8X4),
-                scales=ws[:, lo:lo + cols],
-                in_=gw[(k, g)][:, 4 * c0:4 * (c0 + cols)],
+                out=w_codes[:, at:at + cols].bitcast(FP8X4),
+                scales=w_scales[:, at:at + cols],
+                in_=w_grouped[(k, g)][:, 4 * lo:4 * (lo + cols)],
             )
-            for j in range(c0 // P, (c0 + cols) // P):
-                ready.add((nh, gate, part * 2 + g, j))
-
 
         banks = {}
-        s_t = {}
-        st = {}
+        sigmoids = {}
+        sums = {}
+        gate_out = {}
+        staged = {}
 
-        def mx(nh, gate, h, i, c, c0=0, cw=512):
-            for j in ((i,) if FORM[(nh, h)] == "B" else range(4)):
-                assert (nh, gate, c, j) in ready
-            wl = (gate * 4 + c) * 1024 + nh * 512
-            if FORM[(nh, h)] == "B":
-                a, b = wl + i * P, c * 1024 + h * 512
-                l_c, l_s, r_c, r_s = wq, ws, xq, xs
+        def mx_pass(nh, gate, h, i, lo, cols, c):
+            w_at = (gate * 4 + c) * 1024 + nh * BANK
+            if nh == 0:
+                l_at, r_at = w_at + i * P, c * 1024 + h * BANK
+                l_codes, l_scales, r_codes, r_scales = w_codes, w_scales, x_codes, x_scales
             else:
-                a, b = c * 1024 + (h * 4 + i) * P, wl + c0
-                l_c, l_s, r_c, r_s = xq, xs, wq, ws
+                l_at, r_at = c * 1024 + (h * 4 + i) * P, w_at + lo
+                l_codes, l_scales, r_codes, r_scales = x_codes, x_scales, w_codes, w_scales
             nc.tensor.matmul_mx(
-                out=banks[(h, i, c0)][:, 0:cw],
-                lhsT=l_c[:, a:a + P].bitcast(FP8X4),
-                lhsT_scale=l_s[:, a:a + P],
-                rhs=r_c[:, b:b + cw].bitcast(FP8X4),
-                rhs_scale=r_s[:, b:b + cw],
+                out=banks[(h, i, lo)][:, 0:cols],
+                lhsT=l_codes[:, l_at:l_at + P].bitcast(FP8X4),
+                lhsT_scale=l_scales[:, l_at:l_at + P],
+                rhs=r_codes[:, r_at:r_at + cols].bitcast(FP8X4),
+                rhs_scale=r_scales[:, r_at:r_at + cols],
                 start=(c == 0),
                 stop=(c == 3),
             )
 
-        def store(nh, h, lo, cnt, c0=0, cw=512):
+        def store(nh, h, first, count, lo=0, cols=BANK):
             nc.sync.dma_start(
-                out=ov[:, h * 4 + lo:h * 4 + lo + cnt, nh * 512 + c0:nh * 512 + c0 + cw],
-                in_=st[h][:, lo:lo + cnt, c0:c0 + cw],
+                out=out_rows[:, h * 4 + first:h * 4 + first + count, nh * BANK + lo:nh * BANK + lo + cols],
+                in_=staged[h][:, first:first + count, lo:lo + cols],
             )
 
-        d_t = {}
-        u_t = {}
-
-        def stage1(nh, gate, h, i, c0=0, cw=512):
-            bank = banks[(h, i, c0)]
-            func = ACT.Sigmoid if gate == 0 else ACT.Tanh
-            if FORM[(nh, h)] == "B":
-                if gate == 0:
-                    s_t[(h, i)] = spool.tile([P, 512], F32, name="s", tag="s")
-                    d_t[(h, i, c0)] = s_t[(h, i)]
-                else:
-                    d_t[(h, i, c0)] = gpool.tile([P, 512], F32, name="gt", tag="gt")
-                col = gate * 8 + nh * 4 + i
-                nc.scalar.activation(out=d_t[(h, i, c0)][:], in_=bank[:], func=func, bias=bT[:, col:col + 1])
+        def gate_tile(gate, h, i, lo):
+            if gate == 0:
+                sigmoids[(h, i)] = spool.tile([P, BANK], F32, name="sigmoid", tag="s")
+                gate_out[(h, i, lo)] = sigmoids[(h, i)]
             else:
-                lo = gate * 1024 + nh * 512 + c0
-                u_t[(h, i, c0)] = upool.tile([P, 512], F32, name="u", tag="u")
-                nc.vector.tensor_tensor(out=u_t[(h, i, c0)][:, 0:cw], in0=bank[:, 0:cw], in1=bb[:, lo:lo + cw], op=ALU.add)
+                gate_out[(h, i, lo)] = gpool.tile([P, BANK], F32, name="tanh", tag="gt")
 
-        def stage2(nh, gate, h, i, c0=0, cw=512):
-            func = ACT.Sigmoid if gate == 0 else ACT.Tanh
-            if FORM[(nh, h)] == "B":
-                if gate == 1:
-                    s = s_t[(h, i)]
-                    nc.vector.tensor_tensor(out=s[:], in0=s[:], in1=d_t[(h, i, c0)][:], op=ALU.mult)
+        def step_1(nh, gate, h, i, lo, cols):
+            bank = banks[(h, i, lo)]
+            if nh == 0:
+                gate_tile(gate, h, i, lo)
+                nc.scalar.activation(out=gate_out[(h, i, lo)][:], in_=bank[:], func=ACT.Sigmoid if gate == 0 else ACT.Tanh,
+                                     bias=bias_col[:, 4 * gate + i:4 * gate + i + 1])
             else:
-                if gate == 0:
-                    s_t[(h, i)] = spool.tile([P, 512], F32, name="s", tag="s")
-                    d_t[(h, i, c0)] = s_t[(h, i)]
-                else:
-                    d_t[(h, i, c0)] = gpool.tile([P, 512], F32, name="gt", tag="gt")
-                nc.scalar.activation(out=d_t[(h, i, c0)][:, 0:cw], in_=u_t[(h, i, c0)][:, 0:cw], func=func)
+                at = gate * BANK + lo
+                sums[(h, i, lo)] = upool.tile([P, BANK], F32, name="sum", tag="u")
+                nc.vector.tensor_tensor(out=sums[(h, i, lo)][:, 0:cols], in0=bank[:, 0:cols],
+                                        in1=bias_wide[:, at:at + cols], op=ALU.add)
 
-        def stage3(nh, gate, h, i, c0=0, cw=512):
-            if FORM[(nh, h)] == "A" and gate == 1:
-                eng = nc.gpsimd if (nh * 8 + h * 4 + i) in G_PROD else nc.vector
-                eng.tensor_tensor(out=st[h][:, i, c0:c0 + cw], in0=s_t[(h, i)][:, c0:c0 + cw],
-                                  in1=d_t[(h, i, c0)][:, 0:cw], op=ALU.mult)
-                if cw < 512:
-                    store(nh, h, i, 1, c0, cw)
-                elif (nh * 8 + h * 4 + i) // 2 in SINGLE:
-                    store(nh, h, i, 1)
-                elif i % 2 == 1:
-                    store(nh, h, i - 1, 2)
+        def step_2(nh, gate, h, i, lo, cols):
+            if nh == 0:
+                product = sigmoids[(h, i)]
+                nc.vector.tensor_tensor(out=product[:], in0=product[:], in1=gate_out[(h, i, lo)][:], op=ALU.mult)
+            else:
+                gate_tile(gate, h, i, lo)
+                nc.scalar.activation(out=gate_out[(h, i, lo)][:, 0:cols], in_=sums[(h, i, lo)][:, 0:cols],
+                                     func=ACT.Sigmoid if gate == 0 else ACT.Tanh)
+
+        def step_3(nh, gate, h, i, lo, cols):
+            engine = nc.gpsimd if h * 4 + i < GPSIMD_PRODUCTS else nc.vector
+            engine.tensor_tensor(out=staged[h][:, i, lo:lo + cols], in0=sigmoids[(h, i)][:, lo:lo + cols],
+                                 in1=gate_out[(h, i, lo)][:, 0:cols], op=ALU.mult)
+            store(nh, h, i, 1, lo, cols)
 
         def turn_back(nh, h):
             for tl in range(4):
-                bt = psum.tile([P, 512], F32, name="bt", tag="bank")
+                bank = psum.tile([P, BANK], F32, name="bank_t", tag="bank")
                 for i in range(4):
-                    nc.tensor.transpose(bt[:, i * P:(i + 1) * P], s_t[(h, i)][:, tl * P:(tl + 1) * P], ident[:])
-                if tl in T_ON_V:
-                    nc.vector.tensor_copy(out=st[h][:, tl, :], in_=bt[:])
+                    nc.tensor.transpose(bank[:, i * P:(i + 1) * P], sigmoids[(h, i)][:, tl * P:(tl + 1) * P], ident[:])
+                if tl == VECTOR_BACK_BANK:
+                    nc.vector.tensor_copy(out=staged[h][:, tl, :], in_=bank[:])
                 else:
-                    nc.scalar.copy(out=st[h][:, tl, :], in_=bt[:])
+                    nc.scalar.copy(out=staged[h][:, tl, :], in_=bank[:])
                 if tl % 2 == 1:
                     store(nh, h, tl - 1, 2)
 
-        groups = [(h, i) for h in range(2) for i in range(4)]
-        items = []
+        pairs = [(h, i) for h in range(2) for i in range(4)]
+        visits = []
         for nh in range(2):
             for gate in range(2):
-                if (nh, gate) in SPLIT:
+                if nh == 0:
                     for part in range(2):
-                        for h, i in groups:
-                            items.append((nh, gate, h, i, (2 * part, 2 * part + 1), 0, 512))
+                        for h, i in pairs:
+                            visits.append(((nh, gate, h, i, 0, BANK), (2 * part, 2 * part + 1)))
                 else:
-                    for h, i in groups:
-                        if (nh, gate) == (1, 1) and h * 4 + i >= 8 - TAPER:
-                            items.append((nh, gate, h, i, (0, 1, 2, 3), 0, 256))
-                            items.append((nh, gate, h, i, (0, 1, 2, 3), 256, 256))
+                    for h, i in pairs:
+                        if gate == 1 and h * 4 + i >= 8 - HALVED_GROUPS:
+                            visits.append(((nh, gate, h, i, 0, 256), (0, 1, 2, 3)))
+                            visits.append(((nh, gate, h, i, 256, 256), (0, 1, 2, 3)))
                         else:
-                            items.append((nh, gate, h, i, (0, 1, 2, 3), 0, 512))
+                            visits.append(((nh, gate, h, i, 0, BANK), (0, 1, 2, 3)))
         later = {}
 
-        def defer(n, fn, args):
-            later[n] = later.get(n, []) + [(fn, args)]
+        def defer(n, step, args):
+            later[n] = later.get(n, []) + [(step, args)]
 
         for g in range(2):
             for lo in (0, 256):
                 regroup(0, g, "V", lo, 256)
-                quant(0, g, lo, 256)
-        x_quant(1, 1)
-        subs = [(k, g) for k in range(1, 8) for g in range(2)]
-        n_items = len(items)
-        for n in range(n_items + 8):
-            for kg in subs:
-                if R_AT[kg][0] == n:
-                    if R_AT[kg][1] == "VS":
-                        regroup(kg[0], kg[1], "V", 0, 336)
-                        regroup(kg[0], kg[1], "S", 336, 176)
+                quantise_w(0, g, lo, 256)
+        quantise_x(1, 1)
+
+        sub_blocks = [(k, g) for k in range(1, 8) for g in range(2)]
+        for n in range(len(visits) + TURN_BACK_LAG + 1):
+            for k, g in sub_blocks:
+                if REGROUP_AT[(k, g)][0] == n:
+                    if REGROUP_AT[(k, g)][1] == "VS":
+                        regroup(k, g, "V", 0, VECTOR_SHARE)
+                        regroup(k, g, "S", VECTOR_SHARE, BANK - VECTOR_SHARE)
                     else:
-                        regroup(kg[0], kg[1], R_AT[kg][1])
-            for kg in subs:
-                if Q_AT[kg] == n:
-                    quant(kg[0], kg[1])
-            if n < n_items and items[n][4] == (0, 1):
-                nh, gate, h, i, cs, c0, cw = items[n]
-                if (h, i) == (0, 0):
-                    for h, i in groups:
-                        banks[(h, i, 0)] = psum.tile([P, 512], F32, name="acc", tag="bank")
-                    for c in range(2):
-                        for h, i in sorted(groups, key=lambda hi: hi[1] // 2):
-                            mx(nh, gate, h, i, c)
-            elif n < n_items:
-                nh, gate, h, i, cs, c0, cw = items[n]
-                if cs[0] == 0:
-                    banks[(h, i, c0)] = psum.tile([P, 512], F32, name="acc", tag="bank")
-                if gate == 1 and cs[-1] == 3 and i == 0:
-                    st[h] = stpool.tile([P, 4, 512], F32, name="st", tag="st")
-                for c in cs:
-                    mx(nh, gate, h, i, c, c0, cw)
-                if cs[-1] == 3:
-                    stage1(nh, gate, h, i, c0, cw)
-                    defer(n + LAG1, stage2, (nh, gate, h, i, c0, cw))
-                    defer(n + LAG2, stage3, (nh, gate, h, i, c0, cw))
-                    if gate == 1 and i == 3 and FORM[(nh, h)] == "B":
-                        defer(n + LAG1 + TLAG, turn_back, (nh, h))
-            for fn, args in later.get(n, []):
-                fn(*args)
+                        regroup(k, g, REGROUP_AT[(k, g)][1])
+            for k, g in sub_blocks:
+                if QUANT_AT[(k, g)] == n:
+                    quantise_w(k, g)
+            if n < len(visits):
+                group, passes = visits[n]
+                nh, gate, h, i, lo, cols = group
+                if passes == (0, 1):
+                    if (h, i) == (0, 0):
+                        for h2, i2 in pairs:
+                            banks[(h2, i2, 0)] = psum.tile([P, BANK], F32, name="bank_g", tag="bank")
+                        for c in passes:
+                            for h2, i2 in sorted(pairs, key=lambda hi: hi[1] // 2):
+                                mx_pass(nh, gate, h2, i2, 0, BANK, c)
+                else:
+                    if passes[0] == 0:
+                        banks[(h, i, lo)] = psum.tile([P, BANK], F32, name="bank_g", tag="bank")
+                    if gate == 1 and i == 0:
+                        staged[h] = stpool.tile([P, 4, BANK], F32, name="staged", tag="st")
+                    for c in passes:
+                        mx_pass(nh, gate, h, i, lo, cols, c)
+                    step_1(*group)
+                    if nh == 1 or gate == 1:
+                        defer(n + STEP_2_LAG, step_2, group)
+                    if nh == 1 and gate == 1:
+                        defer(n + STEP_3_LAG, step_3, group)
+                    if nh == 0 and gate == 1 and i == 3:
+                        defer(n + TURN_BACK_LAG, turn_back, (nh, h))
+            for step, args in later.get(n, []):
+                step(*args)

@@ -16,17 +16,10 @@ P = 128
 BANK = 512
 FLOPS = 2 * 1024 * 2048 * 2048
 
-REGROUP_AT = {
-    (1, 0): (0, "S"), (1, 1): (0, "VS"), (2, 0): (4, "V"), (2, 1): (4, "VS"), (3, 0): (17, "VS"), (3, 1): (13, "V"),
-    (4, 0): (17, "VS"), (4, 1): (18, "VS"), (5, 0): (23, "V"), (5, 1): (18, "S"), (6, 0): (32, "S"), (6, 1): (33, "S"),
-    (7, 0): (33, "V"), (7, 1): (30, "V"),
-}
-QUANT_AT = {
-    (1, 0): 0, (1, 1): 1, (2, 0): 4, (2, 1): 14, (3, 0): 18, (3, 1): 16, (4, 0): 21, (4, 1): 23, (5, 0): 25, (5, 1): 25,
-    (6, 0): 36, (6, 1): 36, (7, 0): 35, (7, 1): 35,
-}
-VECTOR_SHARE = 336
-VECTOR_X_BANKS = (3, 4, 7, 10)
+PREP_FIRST = 7
+PREP_STRIDE = 5
+QUANT_LAG = 3
+VECTOR_SHARE = 352
 STEP_2_LAG = 1
 STEP_3_LAG = 3
 TURN_BACK_LAG = 5
@@ -118,7 +111,7 @@ def tile_lstmmirrored_pa_kernel(tc, x, hist, Wix, Wih, b_i, Wcx, Wch, b_c, out):
                 dst = x_grouped[(c, h)][:].bitcast(F32).rearrange("q (c u) -> q c u", u=2)
                 dst = dst[:, (tp % 2) * 256:(tp % 2) * 256 + 256, :]
                 src = bank[:].rearrange("q (u c) -> q c u", u=2)
-                if (si * 8 + tp * 2 + g) in VECTOR_X_BANKS:
+                if (tp * 2 + g) % 4 == 2:
                     nc.vector.tensor_copy(out=dst, in_=src)
                 else:
                     nc.scalar.copy(out=dst, in_=src)
@@ -241,7 +234,7 @@ def tile_lstmmirrored_pa_kernel(tc, x, hist, Wix, Wih, b_i, Wcx, Wch, b_c, out):
                                  in1=gate_out[(h, i, lo)][:, 0:cols], op=ALU.mult)
             store(nh, h, i, 1, lo, cols)
 
-        def turn_back(nh, h):
+        def turn_back(h):
             for tl in range(4):
                 bank = psum.tile([P, BANK], F32, name="bank_t", tag="bank")
                 for i in range(4):
@@ -251,7 +244,7 @@ def tile_lstmmirrored_pa_kernel(tc, x, hist, Wix, Wih, b_i, Wcx, Wch, b_c, out):
                 else:
                     nc.scalar.copy(out=staged[h][:, tl, :], in_=bank[:])
                 if tl % 2 == 1:
-                    store(nh, h, tl - 1, 2)
+                    store(0, h, tl - 1, 2)
 
         pairs = [(h, i) for h in range(2) for i in range(4)]
         visits = []
@@ -268,29 +261,34 @@ def tile_lstmmirrored_pa_kernel(tc, x, hist, Wix, Wih, b_i, Wcx, Wch, b_c, out):
                             visits.append(((nh, gate, h, i, 256, 256), (0, 1, 2, 3)))
                         else:
                             visits.append(((nh, gate, h, i, 0, BANK), (0, 1, 2, 3)))
-        later = {}
 
-        def defer(n, step, args):
-            later[n] = later.get(n, []) + [(step, args)]
+        def closed_at(n):
+            if 0 <= n < len(visits) and visits[n][1][-1] == 3:
+                return visits[n][0]
+            return None
+
+        def shared_regroup(k, g):
+            regroup(k, g, "V", 0, VECTOR_SHARE)
+            regroup(k, g, "S", VECTOR_SHARE, BANK - VECTOR_SHARE)
 
         for g in range(2):
             for lo in (0, 256):
                 regroup(0, g, "V", lo, 256)
                 quantise_w(0, g, lo, 256)
         quantise_x(1, 1)
+        regroup(1, 0, "S")
+        shared_regroup(1, 1)
+        for g in range(2):
+            quantise_w(1, g)
 
-        sub_blocks = [(k, g) for k in range(1, 8) for g in range(2)]
         for n in range(len(visits) + TURN_BACK_LAG + 1):
-            for k, g in sub_blocks:
-                if REGROUP_AT[(k, g)][0] == n:
-                    if REGROUP_AT[(k, g)][1] == "VS":
-                        regroup(k, g, "V", 0, VECTOR_SHARE)
-                        regroup(k, g, "S", VECTOR_SHARE, BANK - VECTOR_SHARE)
-                    else:
-                        regroup(k, g, REGROUP_AT[(k, g)][1])
-            for k, g in sub_blocks:
-                if QUANT_AT[(k, g)] == n:
-                    quantise_w(k, g)
+            for k in range(2, 8):
+                if n == PREP_FIRST + PREP_STRIDE * (k - 2):
+                    for g in range(2):
+                        shared_regroup(k, g)
+                if n == PREP_FIRST + PREP_STRIDE * (k - 2) + QUANT_LAG:
+                    for g in range(2):
+                        quantise_w(k, g)
             if n < len(visits):
                 group, passes = visits[n]
                 nh, gate, h, i, lo, cols = group
@@ -309,11 +307,12 @@ def tile_lstmmirrored_pa_kernel(tc, x, hist, Wix, Wih, b_i, Wcx, Wch, b_c, out):
                     for c in passes:
                         mx_pass(nh, gate, h, i, lo, cols, c)
                     step_1(*group)
-                    if nh == 1 or gate == 1:
-                        defer(n + STEP_2_LAG, step_2, group)
-                    if nh == 1 and gate == 1:
-                        defer(n + STEP_3_LAG, step_3, group)
-                    if nh == 0 and gate == 1 and i == 3:
-                        defer(n + TURN_BACK_LAG, turn_back, (nh, h))
-            for step, args in later.get(n, []):
-                step(*args)
+            group = closed_at(n - TURN_BACK_LAG)
+            if group is not None and group[:2] == (0, 1) and group[3] == 3:
+                turn_back(group[2])
+            group = closed_at(n - STEP_3_LAG)
+            if group is not None and group[:2] == (1, 1):
+                step_3(*group)
+            group = closed_at(n - STEP_2_LAG)
+            if group is not None and group[:2] != (0, 0):
+                step_2(*group)

from contextlib import ExitStack

import concourse.mybir as mybir
from concourse.masks import make_identity

F32 = mybir.dt.float32
BF16 = mybir.dt.bfloat16
U32 = mybir.dt.uint32
U8 = mybir.dt.uint8
I32 = mybir.dt.int32
FP8X4 = mybir.dt.float8_e4m3fn_x4
ACT = mybir.ActivationFunctionType
ALU = mybir.AluOpType

P = 128
BANK = 512
FLOPS = 2 * 1024 * 2048 * 2048

PREP_FIRST = 7
PREP_STRIDE = 5
QUANT_LAG = 3
VECTOR_SHARE = 352
STEP_2_LAG = 1
STEP_3_LAG = 3
TURN_BACK_LAG = 5
VECTOR_BACK_BANK = 1
GPSIMD_PRODUCTS = 5
HALVED_GROUPS = 2


def tile_lstmmirrored_pa_kernel(tc, x, hist, Wix, Wih, b_i, Wcx, Wch, b_c, out):
    nc = tc.nc
    with ExitStack() as ctx:
        ctx.enter_context(tc.manual_schedule())
        const = ctx.enter_context(tc.tile_pool(name="const", bufs=1))
        keep = ctx.enter_context(tc.tile_pool(name="keep", bufs=1))
        raw = ctx.enter_context(tc.tile_pool(name="raw", bufs=8))
        grp = ctx.enter_context(tc.tile_pool(name="grp", bufs=8))
        spool = ctx.enter_context(tc.tile_pool(name="spool", bufs=12))
        gpool = ctx.enter_context(tc.tile_pool(name="gpool", bufs=5))
        upool = ctx.enter_context(tc.tile_pool(name="upool", bufs=4))
        stpool = ctx.enter_context(tc.tile_pool(name="stpool", bufs=2))
        psum = ctx.enter_context(tc.psum_pool(name="psum", bufs=8))

        x_rows = x.rearrange("(p t) k -> p (t k)", t=8)
        hist_rows = hist.rearrange("(p t) k -> p (t k)", t=8)
        out_rows = out.rearrange("(p t) n -> p t n", t=8)
        matrices = ((Wix, Wih), (Wcx, Wch))
        blocks = [(nh, gate, part) for nh in range(2) for gate in range(2) for part in range(2)]

        warm = const.tile([P, 1], F32, name="warm")
        nc.vector.memset(warm[:], 0.0)
        nc.scalar.activation(out=warm[:], in_=warm[:], func=ACT.Sigmoid)
        ident = const.tile([P, P], F32, name="ident")
        make_identity(nc, ident[:])
        bias_row = const.tile([P, 2048], BF16, name="bias_row")
        nc.vector.memset(bias_row[:].bitcast(I32), 0)
        nc.scalar.dma_start(out=bias_row[0:1, 0:1024], in_=b_i.rearrange("(o n) -> o n", o=1))
        nc.scalar.dma_start(out=bias_row[0:1, 1024:2048], in_=b_c.rearrange("(o n) -> o n", o=1))
        ones = const.tile([P, P], BF16, name="ones")
        nc.vector.memset(ones[:], 1.0)
        bias_col = const.tile([P, 8], F32, name="bias_col")
        bias_wide = const.tile([P, 2 * BANK], F32, name="bias_wide")

        x_codes = keep.tile([P, 4 * 1024], U32, name="x_codes", align_bytes=64)
        x_scales = keep.tile([P, 4 * 1024], U8, name="x_scales", align_bytes=64)
        w_codes = keep.tile([P, 8 * 1024], U32, name="w_codes", align_bytes=64)
        w_scales = keep.tile([P, 8 * 1024], U8, name="w_scales", align_bytes=64)

        x_raw = []
        for si, rows in enumerate((x_rows, hist_rows)):
            for h in range(2):
                tile4 = raw.tile([P, 4096], BF16, name="x_raw%d%d" % (si, h), tag="raw")
                for a in range(2):
                    lo = (h * 4 + a * 2) * 1024
                    nc.sync.dma_start(out=tile4[:, a * 2048:(a + 1) * 2048], in_=rows[:, lo:lo + 2048])
                x_raw.append(tile4)

        w_raw = {}

        def load_weights(k):
            nh, gate, part = blocks[k]
            src = matrices[gate][part][:, nh * BANK:(nh + 1) * BANK].rearrange("(a q e) c -> q a e c", a=4, e=2)
            w_raw[k] = raw.tile([P, 4096], BF16, name="w_raw%d" % k, tag="raw")
            dst = w_raw[k][:].rearrange("q (a e c) -> q a e c", a=4, e=2)
            if k < 2:
                for a in range(4):
                    nc.sync.dma_start(out=dst[:, a, :, :], in_=src[:, a, :, :])
            else:
                for e in range(2):
                    nc.sync.dma_start(out=dst[:, :, e, :], in_=src[:, :, e, :])

        for k in range(4):
            load_weights(k)

        x_grouped = {}

        def transpose_pair(si, tp):
            words = x_raw[si * 2 + tp // 2][:].bitcast(F32)
            h = tp // 2
            for g in range(2):
                bank = psum.tile([P, BANK], F32, name="bank_x", tag="bank")
                for u in range(2):
                    for t2 in range(2):
                        w0 = ((tp % 2) * 2 + t2) * 512 + (2 * g + u) * P
                        o0 = (u * 2 + t2) * P
                        nc.tensor.transpose(bank[:, o0:o0 + P], words[:, w0:w0 + P], ident[:])
                c = 2 * si + g
                if tp % 2 == 0:
                    x_grouped[(c, h)] = grp.tile([P, 2048], BF16, name="x_grouped%d%d" % (c, h), tag="grp", align_bytes=64)
                dst = x_grouped[(c, h)][:].bitcast(F32).rearrange("q (c u) -> q c u", u=2)
                dst = dst[:, (tp % 2) * 256:(tp % 2) * 256 + 256, :]
                src = bank[:].rearrange("q (u c) -> q c u", u=2)
                if (tp * 2 + g) % 4 == 2:
                    nc.vector.tensor_copy(out=dst, in_=src)
                else:
                    nc.scalar.copy(out=dst, in_=src)

        def quantise_x(si, h):
            for g in range(2):
                c = 2 * si + g
                lo = c * 1024 + h * BANK
                nc.vector.quantize_mx(
                    out=x_codes[:, lo:lo + BANK].bitcast(FP8X4),
                    scales=x_scales[:, lo:lo + BANK],
                    in_=x_grouped[(c, h)][:],
                )

        for si in range(2):
            for tp in range(4):
                transpose_pair(si, tp)
                if (si, tp) in ((0, 2), (1, 0), (1, 2)):
                    done = si * 4 + tp - 2
                    quantise_x(done // 4, (done % 4) // 2)

        bank = psum.tile([P, BANK], F32, name="bank_b", tag="bank")
        for col in range(8):
            lo = (col // 4) * 1024 + (col % 4) * P
            nc.tensor.matmul(bank[:, col * 32:(col + 1) * 32], lhsT=bias_row[:, lo:lo + P], rhs=ones[:, 0:32],
                             start=True, stop=True)
        nc.scalar.copy(out=bias_col[:], in_=bank[:, 0:256].rearrange("p (c r) -> p c r", r=32)[:, :, 0])
        for gate in range(2):
            bank = psum.tile([P, BANK], F32, name="bank_w", tag="bank")
            lo = gate * 1024 + BANK
            nc.tensor.matmul(bank[:], lhsT=ones[:], rhs=bias_row[:, lo:lo + BANK], start=True, stop=True)
            nc.scalar.copy(out=bias_wide[:, gate * BANK:(gate + 1) * BANK], in_=bank[:])

        for k in range(4, 8):
            load_weights(k)

        w_grouped = {}

        def regroup(k, g, engine, lo=0, cols=BANK):
            if lo == 0:
                w_grouped[(k, g)] = grp.tile([P, 2048], BF16, name="w_grouped%d%d" % (k, g), tag="grp", align_bytes=64)
            dst = w_grouped[(k, g)][:, 4 * lo:4 * (lo + cols)].rearrange("q (c i t) -> q c t i", i=4, t=4)
            src = w_raw[k][:, g * 2048:(g + 1) * 2048].rearrange("q (t n) -> q t n", t=4)
            src = src[:, :, lo:lo + cols].rearrange("q t (c i) -> q c t i", i=4)
            if engine == "S":
                nc.scalar.copy(out=dst, in_=src)
            else:
                nc.vector.tensor_copy(out=dst, in_=src)

        def quantise_w(k, g, lo=0, cols=BANK):
            nh, gate, part = blocks[k]
            at = (gate * 4 + part * 2 + g) * 1024 + nh * BANK + lo
            nc.vector.quantize_mx(
                out=w_codes[:, at:at + cols].bitcast(FP8X4),
                scales=w_scales[:, at:at + cols],
                in_=w_grouped[(k, g)][:, 4 * lo:4 * (lo + cols)],
            )

        banks = {}
        sigmoids = {}
        sums = {}
        gate_out = {}
        staged = {}

        def mx_pass(nh, gate, h, i, lo, cols, c):
            w_at = (gate * 4 + c) * 1024 + nh * BANK
            if nh == 0:
                l_at, r_at = w_at + i * P, c * 1024 + h * BANK
                l_codes, l_scales, r_codes, r_scales = w_codes, w_scales, x_codes, x_scales
            else:
                l_at, r_at = c * 1024 + (h * 4 + i) * P, w_at + lo
                l_codes, l_scales, r_codes, r_scales = x_codes, x_scales, w_codes, w_scales
            nc.tensor.matmul_mx(
                out=banks[(h, i, lo)][:, 0:cols],
                lhsT=l_codes[:, l_at:l_at + P].bitcast(FP8X4),
                lhsT_scale=l_scales[:, l_at:l_at + P],
                rhs=r_codes[:, r_at:r_at + cols].bitcast(FP8X4),
                rhs_scale=r_scales[:, r_at:r_at + cols],
                start=(c == 0),
                stop=(c == 3),
            )

        def store(nh, h, first, count, lo=0, cols=BANK):
            nc.sync.dma_start(
                out=out_rows[:, h * 4 + first:h * 4 + first + count, nh * BANK + lo:nh * BANK + lo + cols],
                in_=staged[h][:, first:first + count, lo:lo + cols],
            )

        def gate_tile(gate, h, i, lo):
            if gate == 0:
                sigmoids[(h, i)] = spool.tile([P, BANK], F32, name="sigmoid", tag="s")
                gate_out[(h, i, lo)] = sigmoids[(h, i)]
            else:
                gate_out[(h, i, lo)] = gpool.tile([P, BANK], F32, name="tanh", tag="gt")

        def step_1(nh, gate, h, i, lo, cols):
            bank = banks[(h, i, lo)]
            if nh == 0:
                gate_tile(gate, h, i, lo)
                nc.scalar.activation(out=gate_out[(h, i, lo)][:], in_=bank[:], func=ACT.Sigmoid if gate == 0 else ACT.Tanh,
                                     bias=bias_col[:, 4 * gate + i:4 * gate + i + 1])
            else:
                at = gate * BANK + lo
                sums[(h, i, lo)] = upool.tile([P, BANK], F32, name="sum", tag="u")
                nc.vector.tensor_tensor(out=sums[(h, i, lo)][:, 0:cols], in0=bank[:, 0:cols],
                                        in1=bias_wide[:, at:at + cols], op=ALU.add)

        def step_2(nh, gate, h, i, lo, cols):
            if nh == 0:
                product = sigmoids[(h, i)]
                nc.vector.tensor_tensor(out=product[:], in0=product[:], in1=gate_out[(h, i, lo)][:], op=ALU.mult)
            else:
                gate_tile(gate, h, i, lo)
                nc.scalar.activation(out=gate_out[(h, i, lo)][:, 0:cols], in_=sums[(h, i, lo)][:, 0:cols],
                                     func=ACT.Sigmoid if gate == 0 else ACT.Tanh)

        def step_3(nh, gate, h, i, lo, cols):
            engine = nc.gpsimd if h * 4 + i < GPSIMD_PRODUCTS else nc.vector
            engine.tensor_tensor(out=staged[h][:, i, lo:lo + cols], in0=sigmoids[(h, i)][:, lo:lo + cols],
                                 in1=gate_out[(h, i, lo)][:, 0:cols], op=ALU.mult)
            store(nh, h, i, 1, lo, cols)

        def turn_back(h):
            for tl in range(4):
                bank = psum.tile([P, BANK], F32, name="bank_t", tag="bank")
                for i in range(4):
                    nc.tensor.transpose(bank[:, i * P:(i + 1) * P], sigmoids[(h, i)][:, tl * P:(tl + 1) * P], ident[:])
                if tl == VECTOR_BACK_BANK:
                    nc.vector.tensor_copy(out=staged[h][:, tl, :], in_=bank[:])
                else:
                    nc.scalar.copy(out=staged[h][:, tl, :], in_=bank[:])
                if tl % 2 == 1:
                    store(0, h, tl - 1, 2)

        pairs = [(h, i) for h in range(2) for i in range(4)]
        visits = []
        for nh in range(2):
            for gate in range(2):
                if nh == 0:
                    for part in range(2):
                        for h, i in pairs:
                            visits.append(((nh, gate, h, i, 0, BANK), (2 * part, 2 * part + 1)))
                else:
                    for h, i in pairs:
                        if gate == 1 and h * 4 + i >= 8 - HALVED_GROUPS:
                            visits.append(((nh, gate, h, i, 0, 256), (0, 1, 2, 3)))
                            visits.append(((nh, gate, h, i, 256, 256), (0, 1, 2, 3)))
                        else:
                            visits.append(((nh, gate, h, i, 0, BANK), (0, 1, 2, 3)))

        def closed_at(n):
            if 0 <= n < len(visits) and visits[n][1][-1] == 3:
                return visits[n][0]
            return None

        def shared_regroup(k, g):
            regroup(k, g, "V", 0, VECTOR_SHARE)
            regroup(k, g, "S", VECTOR_SHARE, BANK - VECTOR_SHARE)

        for g in range(2):
            for lo in (0, 256):
                regroup(0, g, "V", lo, 256)
                quantise_w(0, g, lo, 256)
        quantise_x(1, 1)
        regroup(1, 0, "S")
        shared_regroup(1, 1)
        for g in range(2):
            quantise_w(1, g)

        for n in range(len(visits) + TURN_BACK_LAG + 1):
            for k in range(2, 8):
                if n == PREP_FIRST + PREP_STRIDE * (k - 2):
                    for g in range(2):
                        shared_regroup(k, g)
                if n == PREP_FIRST + PREP_STRIDE * (k - 2) + QUANT_LAG:
                    for g in range(2):
                        quantise_w(k, g)
            if n < len(visits):
                group, passes = visits[n]
                nh, gate, h, i, lo, cols = group
                if passes == (0, 1):
                    if (h, i) == (0, 0):
                        for h2, i2 in pairs:
                            banks[(h2, i2, 0)] = psum.tile([P, BANK], F32, name="bank_g", tag="bank")
                        for c in passes:
                            for h2, i2 in sorted(pairs, key=lambda hi: hi[1] // 2):
                                mx_pass(nh, gate, h2, i2, 0, BANK, c)
                else:
                    if passes[0] == 0:
                        banks[(h, i, lo)] = psum.tile([P, BANK], F32, name="bank_g", tag="bank")
                    if gate == 1 and i == 0:
                        staged[h] = stpool.tile([P, 4, BANK], F32, name="staged", tag="st")
                    for c in passes:
                        mx_pass(nh, gate, h, i, lo, cols, c)
                    step_1(*group)
            group = closed_at(n - TURN_BACK_LAG)
            if group is not None and group[:2] == (0, 1) and group[3] == 3:
                turn_back(group[2])
            group = closed_at(n - STEP_3_LAG)
            if group is not None and group[:2] == (1, 1):
                step_3(*group)
            group = closed_at(n - STEP_2_LAG)
            if group is not None and group[:2] != (0, 0):
                step_2(*group)
